import numpy as np
import ml_dtypes


def mxq(x, axis, fmt="e4m3"):
    dtype, down = {"e4m3": (ml_dtypes.float8_e4m3fn, 7), "e5m2": (ml_dtypes.float8_e5m2, 14)}[fmt]
    v = np.moveaxis(np.asarray(x, np.float32).astype(ml_dtypes.bfloat16).astype(np.float64), axis, -1)
    blocks = v.reshape(v.shape[:-1] + (-1, 32))
    amax = np.abs(blocks).max(-1, keepdims=True)
    byte = np.maximum(np.where(amax > 0, np.frexp(amax)[1] - 1 + 127, 0) - down, 1)
    scale = np.exp2(byte - 127.0)
    codes = (blocks / scale).astype(np.float32).astype(dtype).astype(np.float64)
    return np.moveaxis((codes * scale).reshape(v.shape), -1, axis)


WIDE = False


def mx_kscale(k):
    if not WIDE:
        return np.ones(k)
    levels = np.array([10, -10, 5, -5, 0])
    if k % 512:
        return np.exp2(np.random.permutation(np.resize(levels, k // 32))).repeat(32)
    a = np.empty((k // 512, 16))
    for p in range(k // 512):
        a[p, :8] = np.random.permutation(np.resize(levels, 8))
        for g in range(8):
            far = levels[np.abs(levels - a[p, g]) >= 10]
            a[p, g + 8] = far[np.random.randint(len(far))]
    return np.exp2(a.ravel()).repeat(32)


BF16 = ml_dtypes.bfloat16


def bf(x):
    return np.asarray(x, np.float32).astype(BF16)


def f64(x):
    return np.asarray(x).astype(np.float64)


B, S, HID, NH, NOPE, ROPE, VD, KV_RANK, SW, QB = 1, 8192, 512, 2, 64, 128, 128, 512, 384, 128


def rotate_half(x):
    h = x.shape[-1] // 2
    return np.concatenate([-x[..., h:], x[..., :h]], axis=-1)


def rope_tables():
    pos = np.arange(S, dtype=np.float64)
    inv = 1.0 / (10000.0 ** (np.arange(0, ROPE, 2, dtype=np.float64) / ROPE))
    ang = pos[:, None] * inv[None, :]
    ang = np.concatenate([ang, ang], axis=-1)
    return bf(np.broadcast_to(np.cos(ang)[None], (B, S, ROPE))), bf(np.broadcast_to(np.sin(ang)[None], (B, S, ROPE)))


def setup_inputs():
    s, t = mx_kscale(HID), mx_kscale(KV_RANK)
    col = np.concatenate([t, np.ones(ROPE)])
    cos, sin = rope_tables()
    return {"hidden_states": bf(np.random.standard_normal((B, S, HID)) * s), "cos": cos, "sin": sin,
            "Wkva": bf(np.random.standard_normal((HID, KV_RANK + ROPE)) / np.sqrt(HID) / s[:, None] * col),
            "bkva": bf(np.random.standard_normal(KV_RANK + ROPE) * 0.1 * col),
            "Wkvb": bf(np.random.standard_normal((KV_RANK, NH * (NOPE + VD))) / np.sqrt(KV_RANK) / t[:, None])}


def reference(hidden_states, cos, sin, Wkva, bkva, Wkvb):
    ckv = (mxq(f64(hidden_states), 2, "e4m3") @ mxq(f64(Wkva), 0, "e4m3")) + f64(bkva)
    kv_lat, k_rope = ckv[..., :KV_RANK], ckv[..., KV_RANK:]
    kv = (mxq(kv_lat, 2, "e4m3") @ mxq(f64(Wkvb), 0, "e4m3")).reshape(B, S, NH, NOPE + VD).transpose(0, 2, 1, 3)
    k_nope, v = kv[..., :NOPE], kv[..., NOPE:]
    k_rope = k_rope.reshape(B, 1, S, ROPE)
    c, si = f64(cos)[:, None], f64(sin)[:, None]
    k_rope = k_rope * c + rotate_half(k_rope) * si
    k_rope = np.broadcast_to(k_rope, (B, NH, S, ROPE))
    kk = np.concatenate([k_nope, k_rope], axis=-1)
    return kk, np.ascontiguousarray(v)

@@ -1,0 +1,365 @@
+from contextlib import ExitStack
+
+import concourse.mybir as mybir
+from concourse.masks import make_identity
+
+F32 = mybir.dt.float32
+BF16 = mybir.dt.bfloat16
+U32 = mybir.dt.uint32
+U8 = mybir.dt.uint8
+FP8X4 = mybir.dt.float8_e4m3fn_x4
+ADD = mybir.AluOpType.add
+SUB = mybir.AluOpType.subtract
+MUL = mybir.AluOpType.mult
+
+P = 128
+PACK = 4
+TOKENS = 8192
+HID = 512
+LATENT = 512
+ROPE = 128
+HALF = ROPE // 2
+NOPE = 64
+VDIM = 128
+HEADS = 2
+KK = NOPE + ROPE
+
+TILES = TOKENS // P
+ROUND = 4
+ROUNDS = TILES // ROUND
+CHUNK = 2 * ROUND
+CHUNKS = TILES // CHUNK
+FILL_STEPS = 3
+
+FLOPS = 2 * TOKENS * HID * (LATENT + ROPE) + 2 * TOKENS * LATENT * HEADS * (NOPE + VDIM)
+
+
+def tile_gptossmlaattention_pa_t_kernel(
+    tc, hidden_states, cos, sin, Wkva, bkva, Wkvb, out_0, out_1
+):
+    nc = tc.nc
+    with ExitStack() as ctx:
+        keep = ctx.enter_context(tc.tile_pool(name="keep", bufs=1))
+        work = ctx.enter_context(tc.tile_pool(name="work", bufs=2))
+        psum = ctx.enter_context(tc.psum_pool(name="psum", bufs=4))
+        ctx.enter_context(tc.manual_schedule())
+
+        hs_view = hidden_states.flatten_outer_dims().rearrange("(p n) k -> p n k", n=TILES)
+        cos_view = cos.flatten_outer_dims().rearrange("(p n) d -> p n d", n=TILES)
+        sin_view = sin.flatten_outer_dims().rearrange("(p n) d -> p n d", n=TILES)
+        kk_view = out_0.rearrange("b h (p n) d -> p (b h) n d", n=TILES)
+        v_view = out_1.rearrange("b h (p n) d -> p (b h) n d", n=TILES)
+
+        hs_sb = [keep.tile([P, ROUND, HID], BF16, name="hs%d" % r) for r in range(ROUNDS)]
+        cos_sb = [keep.tile([P, CHUNK, ROPE], BF16, name="cos%d" % c) for c in range(CHUNKS)]
+        sin_sb = [keep.tile([P, CHUNK, ROPE], BF16, name="sin%d" % c) for c in range(CHUNKS)]
+        bias_lat = keep.tile([P, PACK], BF16, name="bias_lat")
+        bias_rope = keep.tile([P, ROPE], BF16, name="bias_rope")
+        ident = keep.tile([P, P], F32, name="ident")
+        wa_codes = keep.tile([P, LATENT + ROPE], U32, name="wa_codes", align_bytes=64)
+        wa_scales = keep.tile([P, LATENT + ROPE], U8, name="wa_scales", align_bytes=64)
+        wb_codes = keep.tile([P, HEADS * (NOPE + VDIM)], U32, name="wb_codes", align_bytes=64)
+        wb_scales = keep.tile([P, HEADS * (NOPE + VDIM)], U8, name="wb_scales", align_bytes=64)
+        LAT_COLS = slice(0, LATENT)
+        ROPE_COLS = slice(LATENT, LATENT + ROPE)
+        V_COLS = slice(0, HEADS * VDIM)
+        NOPE_COLS = slice(HEADS * VDIM, HEADS * (VDIM + NOPE))
+
+        make_identity(nc, ident[:])
+
+        with tc.tile_pool(name="setup", bufs=1) as setup:
+            wa_raw = setup.tile([P, PACK, LATENT + ROPE], BF16, name="wa_raw")
+            nc.sync.dma_start(out=wa_raw[:], in_=Wkva.rearrange("(p j) c -> p j c", j=PACK))
+            wb_raw = setup.tile([P, PACK, HEADS * (NOPE + VDIM)], BF16, name="wb_raw")
+            nc.sync.dma_start(out=wb_raw[:], in_=Wkvb.rearrange("(p j) c -> p j c", j=PACK))
+
+            def load_hidden(c):
+                for r in (2 * c, 2 * c + 1):
+                    tiles = slice(r * ROUND, (r + 1) * ROUND)
+                    nc.sync.dma_start(out=hs_sb[r][:], in_=hs_view[:, tiles, :])
+
+            load_hidden(0)
+            nc.sync.dma_start(out=bias_rope[:], in_=bkva[ROPE_COLS].partition_broadcast(P))
+            nc.sync.dma_start(
+                out=bias_lat[:], in_=bkva[LAT_COLS].rearrange("(m t) -> m t", t=PACK)
+            )
+            load_hidden(1)
+            for c in range(CHUNKS):
+                if c + 2 < CHUNKS:
+                    load_hidden(c + 2)
+                tiles = slice(c * CHUNK, (c + 1) * CHUNK)
+                nc.sync.dma_start(out=cos_sb[c][:], in_=cos_view[:, tiles, :])
+                nc.sync.dma_start(out=sin_sb[c][:], in_=sin_view[:, tiles, :])
+
+            wa_grp = setup.tile([P, LATENT + ROPE, PACK], BF16, name="wa_grp", align_bytes=64)
+            wb_grp = setup.tile(
+                [P, HEADS * (NOPE + VDIM), PACK], BF16, name="wb_grp", align_bytes=64
+            )
+            nc.vector.tensor_copy(
+                out=wa_grp[:, LAT_COLS, :].rearrange("p (t m) j -> p t m j", t=PACK),
+                in_=wa_raw[:, :, LAT_COLS].rearrange("p j (m t) -> p t m j", t=PACK),
+            )
+            nc.vector.tensor_copy(
+                out=wa_grp[:, ROPE_COLS, :], in_=wa_raw[:, :, ROPE_COLS].rearrange("p j c -> p c j")
+            )
+            for cols in (LAT_COLS, ROPE_COLS):
+                nc.vector.quantize_mx(
+                    out=wa_codes[:, cols].bitcast(FP8X4),
+                    scales=wa_scales[:, cols],
+                    in_=wa_grp[:, cols, :].rearrange("p c j -> p (c j)"),
+                )
+            wb_by_head = wb_raw[:].rearrange("p j (h c) -> p h c j", h=HEADS)
+            nc.vector.tensor_copy(
+                out=wb_grp[:, V_COLS, :].rearrange("p (h c) j -> p h c j", h=HEADS),
+                in_=wb_by_head[:, :, NOPE:, :],
+            )
+            nc.vector.tensor_copy(
+                out=wb_grp[:, NOPE_COLS, :].rearrange("p (h c) j -> p h c j", h=HEADS),
+                in_=wb_by_head[:, :, 0:NOPE, :],
+            )
+            for cols in (V_COLS, NOPE_COLS):
+                nc.vector.quantize_mx(
+                    out=wb_codes[:, cols].bitcast(FP8X4),
+                    scales=wb_scales[:, cols],
+                    in_=wb_grp[:, cols, :].rearrange("p c j -> p (c j)"),
+                )
+
+        stage = ctx.enter_context(tc.tile_pool(name="stage", bufs=3))
+
+        hs_grouped = {}
+        hs_mx = {}
+        lat_bank = {}
+        lat_grouped = {}
+        lat_mx = {}
+        rope_bank = {}
+        rope_key = {}
+        key_cos = {}
+        key_sin = {}
+        kk_sb = {}
+        v_sb = {}
+
+        def live(r):
+            return 0 <= r < ROUNDS
+
+        def transpose_hidden(r):
+            if not live(r):
+                return
+            hs_grouped[r] = work.tile(
+                [P, ROUND * P * PACK], BF16, name="hs_grouped", tag="hs_grouped", bufs=4,
+                align_bytes=64,
+            )
+            words = hs_grouped[r][:].bitcast(F32).rearrange("p (i k u) -> p i k u", i=ROUND, u=2)
+            for half in range(ROUND // 2):
+                bank = psum.tile([P, 2, 2, P], F32, name="hs_bank", tag="scalar_ring")
+                for i in range(2):
+                    row_words = hs_sb[r][:, 2 * half + i, :].bitcast(F32)
+                    for u in range(2):
+                        nc.tensor.transpose(
+                            bank[:, i, u, :], row_words[:, u : HID // 2 : 2], ident[:]
+                        )
+                nc.scalar.copy(
+                    out=words[:, 2 * half : 2 * half + 2, :, :],
+                    in_=bank[:].rearrange("p i u k -> p i k u"),
+                )
+
+        def quantise_hidden(r):
+            if not live(r):
+                return
+            codes = work.tile(
+                [P, ROUND * P], U32, name="hs_codes", tag="hs_codes", bufs=4, align_bytes=64
+            )
+            scales = work.tile(
+                [P, ROUND * P], U8, name="hs_scales", tag="hs_scales", bufs=4, align_bytes=64
+            )
+            nc.vector.quantize_mx(
+                out=codes[:].bitcast(FP8X4), scales=scales[:], in_=hs_grouped[r][:]
+            )
+            hs_mx[r] = (codes, scales)
+
+        def latent_matmuls(r, i):
+            if not live(r):
+                return
+            codes, scales = hs_mx[r]
+            bank = psum.tile([P, PACK, P], F32, name="lat_bank", tag="vector_ring")
+            lat_bank[(r, i)] = bank
+            tokens = slice(i * P, (i + 1) * P)
+            for t in range(PACK):
+                cols = slice(t * P, (t + 1) * P)
+                nc.tensor.matmul_mx(
+                    out=bank[:, t, :],
+                    lhsT=wa_codes[:, cols].bitcast(FP8X4),
+                    lhsT_scale=wa_scales[:, cols],
+                    rhs=codes[:, tokens].bitcast(FP8X4),
+                    rhs_scale=scales[:, tokens],
+                    start=True,
+                    stop=True,
+                )
+
+        def latent_out(r, i):
+            if not live(r):
+                return
+            if i == 0:
+                lat_grouped[r] = work.tile(
+                    [P, ROUND, P, PACK], BF16, name="lat_grouped", tag="lat_grouped",
+                    align_bytes=64,
+                )
+            nc.vector.tensor_tensor(
+                out=lat_grouped[r][:, i, :, :],
+                in0=lat_bank[(r, i)][:].rearrange("p t k -> p k t"),
+                in1=bias_lat[:].unsqueeze(1).to_broadcast([P, P, PACK]),
+                op=ADD,
+            )
+
+        def quantise_latent(r):
+            if not live(r):
+                return
+            codes = work.tile([P, ROUND * P], U32, name="lat_codes", tag="lat_codes", align_bytes=64)
+            scales = work.tile(
+                [P, ROUND * P], U8, name="lat_scales", tag="lat_scales", align_bytes=64
+            )
+            nc.vector.quantize_mx(
+                out=codes[:].bitcast(FP8X4),
+                scales=scales[:],
+                in_=lat_grouped[r][:].rearrange("p i k t -> p (i k t)"),
+            )
+            lat_mx[r] = (codes, scales)
+
+        def rope_matmuls(r):
+            if not live(r):
+                return
+            codes, scales = hs_mx[r]
+            bank = psum.tile([P, ROUND, ROPE], F32, name="rope_bank", tag="vector_ring")
+            rope_bank[r] = bank
+            for i in range(ROUND):
+                tokens = slice(i * P, (i + 1) * P)
+                nc.tensor.matmul_mx(
+                    out=bank[:, i, :],
+                    lhsT=codes[:, tokens].bitcast(FP8X4),
+                    lhsT_scale=scales[:, tokens],
+                    rhs=wa_codes[:, ROPE_COLS].bitcast(FP8X4),
+                    rhs_scale=wa_scales[:, ROPE_COLS],
+                    start=True,
+                    stop=True,
+                )
+
+        def rope_out(r):
+            if not live(r):
+                return
+            c, j = divmod(r * ROUND, CHUNK)
+            if j == 0:
+                rope_key[c] = work.tile([P, CHUNK, ROPE], F32, name="rope_key", tag="rope_key")
+            nc.vector.tensor_tensor(
+                out=rope_key[c][:, j : j + ROUND, :],
+                in0=rope_bank[r][:],
+                in1=bias_rope[:].unsqueeze(1).to_broadcast([P, ROUND, ROPE]),
+                op=ADD,
+            )
+
+        low, high = slice(0, HALF), slice(HALF, ROPE)
+
+        def rotate_products(c):
+            if not 0 <= c < CHUNKS:
+                return
+            key = rope_key[c]
+            key_cos[c] = work.tile([P, CHUNK, ROPE], F32, name="key_cos", tag="key_cos", bufs=1)
+            key_sin[c] = work.tile([P, CHUNK, ROPE], F32, name="key_sin", tag="key_sin", bufs=1)
+            nc.gpsimd.tensor_tensor(out=key_cos[c][:], in0=key[:], in1=cos_sb[c][:], op=MUL)
+            nc.gpsimd.tensor_tensor(
+                out=key_sin[c][:, :, low], in0=key[:, :, high], in1=sin_sb[c][:, :, low], op=MUL
+            )
+            nc.gpsimd.tensor_tensor(
+                out=key_sin[c][:, :, high], in0=key[:, :, low], in1=sin_sb[c][:, :, high], op=MUL
+            )
+
+        def rotate_sum(c):
+            if not 0 <= c < CHUNKS:
+                return
+            kk_sb[c] = stage.tile([P, HEADS, CHUNK, KK], F32, name="kk_sb", tag="kk_sb")
+            nc.vector.tensor_tensor(
+                out=kk_sb[c][:, 1, :, NOPE : NOPE + HALF],
+                in0=key_cos[c][:, :, low],
+                in1=key_sin[c][:, :, low],
+                op=SUB,
+            )
+            nc.vector.tensor_tensor(
+                out=kk_sb[c][:, 1, :, NOPE + HALF :],
+                in0=key_cos[c][:, :, high],
+                in1=key_sin[c][:, :, high],
+                op=ADD,
+            )
+
+        def second_product(r):
+            if not live(r):
+                return
+            codes, scales = lat_mx[r]
+            c, j = divmod(r * ROUND, CHUNK)
+            if j == 0:
+                v_sb[c] = stage.tile([P, HEADS, CHUNK, VDIM], F32, name="v_sb", tag="v_sb")
+            for half in range(ROUND // 2):
+                bank = psum.tile([P, 2, HEADS, VDIM], F32, name="v_bank", tag="scalar_ring")
+                for i in range(2):
+                    tokens = slice((2 * half + i) * P, (2 * half + i + 1) * P)
+                    nc.tensor.matmul_mx(
+                        out=bank[:, i, :, :].rearrange("p h d -> p (h d)"),
+                        lhsT=codes[:, tokens].bitcast(FP8X4),
+                        lhsT_scale=scales[:, tokens],
+                        rhs=wb_codes[:, V_COLS].bitcast(FP8X4),
+                        rhs_scale=wb_scales[:, V_COLS],
+                        start=True,
+                        stop=True,
+                    )
+                first = j + 2 * half
+                nc.scalar.copy(
+                    out=v_sb[c][:, :, first : first + 2, :].rearrange("p h i d -> p i h d"),
+                    in_=bank[:],
+                )
+            bank = psum.tile([P, ROUND, HEADS, NOPE], F32, name="nope_bank", tag="scalar_ring")
+            for i in range(ROUND):
+                tokens = slice(i * P, (i + 1) * P)
+                nc.tensor.matmul_mx(
+                    out=bank[:, i, :, :].rearrange("p h d -> p (h d)"),
+                    lhsT=codes[:, tokens].bitcast(FP8X4),
+                    lhsT_scale=scales[:, tokens],
+                    rhs=wb_codes[:, NOPE_COLS].bitcast(FP8X4),
+                    rhs_scale=wb_scales[:, NOPE_COLS],
+                    start=True,
+                    stop=True,
+                )
+            nc.scalar.copy(
+                out=kk_sb[c][:, :, j : j + ROUND, 0:NOPE].rearrange("p h i d -> p i h d"),
+                in_=bank[:],
+            )
+            nc.scalar.copy(
+                out=kk_sb[c][:, 0, j : j + ROUND, NOPE:], in_=kk_sb[c][:, 1, j : j + ROUND, NOPE:]
+            )
+            tiles = slice(r * ROUND, (r + 1) * ROUND)
+            nc.sync.dma_start(out=v_view[:, :, tiles, :], in_=v_sb[c][:, :, j : j + ROUND, :])
+            nc.sync.dma_start(out=kk_view[:, :, tiles, :], in_=kk_sb[c][:, :, j : j + ROUND, :])
+
+        for c in range(-FILL_STEPS, CHUNKS + 1):
+            a, b = 2 * c, 2 * c + 1
+            second_product(a - 2)
+            second_product(b - 2)
+            rotate_products(c)
+            for i in range(ROUND):
+                latent_out(a, i)
+                latent_matmuls(b, i)
+            latent_out(b, 0)
+            rope_matmuls(a + 2)
+            latent_out(b, 1)
+            rope_matmuls(b + 2)
+            latent_out(b, 2)
+            latent_matmuls(a + 2, 0)
+            latent_out(b, 3)
+            latent_matmuls(a + 2, 1)
+            rope_out(a + 2)
+            latent_matmuls(a + 2, 2)
+            rope_out(b + 2)
+            latent_matmuls(a + 2, 3)
+            transpose_hidden(a + 6)
+            transpose_hidden(b + 6)
+            quantise_latent(a)
+            quantise_latent(b)
+            quantise_hidden(a + 4)
+            quantise_hidden(b + 4)
+            rotate_sum(c)

@@ -8,8 +8,8 @@ BF16 = mybir.dt.bfloat16
 U32 = mybir.dt.uint32
 U8 = mybir.dt.uint8
 FP8X4 = mybir.dt.float8_e4m3fn_x4
+IDENTITY = mybir.ActivationFunctionType.Identity
 ADD = mybir.AluOpType.add
-SUB = mybir.AluOpType.subtract
 MUL = mybir.AluOpType.mult
 
 P = 128
@@ -54,7 +54,7 @@ def tile_gptossmlaattention_pa_t_kernel(
         cos_sb = [keep.tile([P, CHUNK, ROPE], BF16, name="cos%d" % c) for c in range(CHUNKS)]
         sin_sb = [keep.tile([P, CHUNK, ROPE], BF16, name="sin%d" % c) for c in range(CHUNKS)]
         bias_lat = keep.tile([P, PACK], BF16, name="bias_lat")
-        bias_rope = keep.tile([P, ROPE], BF16, name="bias_rope")
+        bias_rope = keep.tile([P, 1], BF16, name="bias_rope")
         ident = keep.tile([P, P], F32, name="ident")
         wa_codes = keep.tile([P, LATENT + ROPE], U32, name="wa_codes", align_bytes=64)
         wa_scales = keep.tile([P, LATENT + ROPE], U8, name="wa_scales", align_bytes=64)
@@ -67,255 +67,225 @@ def tile_gptossmlaattention_pa_t_kernel(
 
         make_identity(nc, ident[:])
 
-        with tc.tile_pool(name="setup", bufs=1) as setup:
-            wa_raw = setup.tile([P, PACK, LATENT + ROPE], BF16, name="wa_raw")
-            nc.sync.dma_start(out=wa_raw[:], in_=Wkva.rearrange("(p j) c -> p j c", j=PACK))
-            wb_raw = setup.tile([P, PACK, HEADS * (NOPE + VDIM)], BF16, name="wb_raw")
-            nc.sync.dma_start(out=wb_raw[:], in_=Wkvb.rearrange("(p j) c -> p j c", j=PACK))
-
-            def load_hidden(c):
-                for r in (2 * c, 2 * c + 1):
-                    tiles = slice(r * ROUND, (r + 1) * ROUND)
-                    nc.sync.dma_start(out=hs_sb[r][:], in_=hs_view[:, tiles, :])
-
-            load_hidden(0)
-            nc.sync.dma_start(out=bias_rope[:], in_=bkva[ROPE_COLS].partition_broadcast(P))
-            nc.sync.dma_start(
-                out=bias_lat[:], in_=bkva[LAT_COLS].rearrange("(m t) -> m t", t=PACK)
-            )
-            load_hidden(1)
-            for c in range(CHUNKS):
-                if c + 2 < CHUNKS:
-                    load_hidden(c + 2)
-                tiles = slice(c * CHUNK, (c + 1) * CHUNK)
-                nc.sync.dma_start(out=cos_sb[c][:], in_=cos_view[:, tiles, :])
-                nc.sync.dma_start(out=sin_sb[c][:], in_=sin_view[:, tiles, :])
-
-            wa_grp = setup.tile([P, LATENT + ROPE, PACK], BF16, name="wa_grp", align_bytes=64)
-            wb_grp = setup.tile(
-                [P, HEADS * (NOPE + VDIM), PACK], BF16, name="wb_grp", align_bytes=64
-            )
-            nc.vector.tensor_copy(
-                out=wa_grp[:, LAT_COLS, :].rearrange("p (t m) j -> p t m j", t=PACK),
-                in_=wa_raw[:, :, LAT_COLS].rearrange("p j (m t) -> p t m j", t=PACK),
-            )
-            nc.vector.tensor_copy(
-                out=wa_grp[:, ROPE_COLS, :], in_=wa_raw[:, :, ROPE_COLS].rearrange("p j c -> p c j")
-            )
-            for cols in (LAT_COLS, ROPE_COLS):
-                nc.vector.quantize_mx(
-                    out=wa_codes[:, cols].bitcast(FP8X4),
-                    scales=wa_scales[:, cols],
-                    in_=wa_grp[:, cols, :].rearrange("p c j -> p (c j)"),
-                )
-            wb_by_head = wb_raw[:].rearrange("p j (h c) -> p h c j", h=HEADS)
-            nc.vector.tensor_copy(
-                out=wb_grp[:, V_COLS, :].rearrange("p (h c) j -> p h c j", h=HEADS),
-                in_=wb_by_head[:, :, NOPE:, :],
-            )
-            nc.vector.tensor_copy(
-                out=wb_grp[:, NOPE_COLS, :].rearrange("p (h c) j -> p h c j", h=HEADS),
-                in_=wb_by_head[:, :, 0:NOPE, :],
-            )
-            for cols in (V_COLS, NOPE_COLS):
-                nc.vector.quantize_mx(
-                    out=wb_codes[:, cols].bitcast(FP8X4),
-                    scales=wb_scales[:, cols],
-                    in_=wb_grp[:, cols, :].rearrange("p c j -> p (c j)"),
-                )
-
-        stage = ctx.enter_context(tc.tile_pool(name="stage", bufs=3))
-
         hs_grouped = {}
         hs_mx = {}
         lat_bank = {}
         lat_grouped = {}
         lat_mx = {}
-        rope_bank = {}
-        rope_key = {}
+        key_by_dim = {}
+        key_bank = {}
+        key_swapped = {}
         key_cos = {}
         key_sin = {}
         kk_sb = {}
         v_sb = {}
 
-        def live(r):
-            return 0 <= r < ROUNDS
+        low, high = slice(0, HALF), slice(HALF, ROPE)
+        ROPE_DIMS = slice(NOPE, KK)
 
-        def transpose_hidden(r):
-            if not live(r):
+        def live(c):
+            return 0 <= c < CHUNKS
+
+        def columns(i, count=1):
+            return slice(i * P, (i + count) * P)
+
+        def tiles_of(half):
+            return slice(half * ROUND, (half + 1) * ROUND)
+
+        def transpose_hidden(c, pair):
+            if not live(c):
                 return
-            hs_grouped[r] = work.tile(
-                [P, ROUND * P * PACK], BF16, name="hs_grouped", tag="hs_grouped", bufs=4,
-                align_bytes=64,
-            )
-            words = hs_grouped[r][:].bitcast(F32).rearrange("p (i k u) -> p i k u", i=ROUND, u=2)
-            for half in range(ROUND // 2):
-                bank = psum.tile([P, 2, 2, P], F32, name="hs_bank", tag="scalar_ring")
-                for i in range(2):
-                    row_words = hs_sb[r][:, 2 * half + i, :].bitcast(F32)
-                    for u in range(2):
-                        nc.tensor.transpose(
-                            bank[:, i, u, :], row_words[:, u : HID // 2 : 2], ident[:]
-                        )
-                nc.scalar.copy(
-                    out=words[:, 2 * half : 2 * half + 2, :, :],
-                    in_=bank[:].rearrange("p i u k -> p i k u"),
+            if pair == 0:
+                hs_grouped[c] = work.tile(
+                    [P, CHUNK * P * PACK], BF16, name="hs_grouped", tag="hs_grouped", align_bytes=64
                 )
+            words = hs_grouped[c][:].bitcast(F32).rearrange("p (i k u) -> p i k u", i=CHUNK, u=2)
+            bank = psum.tile([P, 2, 2, P], F32, name="hs_bank", tag="scalar_ring")
+            for i in range(2):
+                r, j = divmod(c * CHUNK + 2 * pair + i, ROUND)
+                row_words = hs_sb[r][:, j, :].bitcast(F32)
+                for u in range(2):
+                    nc.tensor.transpose(bank[:, i, u, :], row_words[:, u : HID // 2 : 2], ident[:])
+            nc.scalar.copy(
+                out=words[:, 2 * pair : 2 * pair + 2, :, :],
+                in_=bank[:].rearrange("p i u k -> p i k u"),
+            )
 
-        def quantise_hidden(r):
-            if not live(r):
-                return
-            codes = work.tile(
-                [P, ROUND * P], U32, name="hs_codes", tag="hs_codes", bufs=4, align_bytes=64
-            )
-            scales = work.tile(
-                [P, ROUND * P], U8, name="hs_scales", tag="hs_scales", bufs=4, align_bytes=64
-            )
+        def quantise(grouped, done, c, halves):
+            codes, scales = done[c]
+            tokens = slice(halves[0] * ROUND * P, (halves[-1] + 1) * ROUND * P)
+            values = slice(tokens.start * PACK, tokens.stop * PACK)
             nc.vector.quantize_mx(
-                out=codes[:].bitcast(FP8X4), scales=scales[:], in_=hs_grouped[r][:]
+                out=codes[:, tokens].bitcast(FP8X4),
+                scales=scales[:, tokens],
+                in_=grouped[c][:, values],
             )
-            hs_mx[r] = (codes, scales)
 
-        def latent_matmuls(r, i):
-            if not live(r):
+        def quantise_hidden(c, halves=(0, 1)):
+            if not live(c):
                 return
-            codes, scales = hs_mx[r]
+            if halves[0] == 0:
+                codes = work.tile(
+                    [P, CHUNK * P], U32, name="hs_codes", tag="hs_codes", align_bytes=64
+                )
+                scales = work.tile(
+                    [P, CHUNK * P], U8, name="hs_scales", tag="hs_scales", align_bytes=64
+                )
+                hs_mx[c] = (codes, scales)
+            quantise(hs_grouped, hs_mx, c, halves)
+
+        def latent_matmuls(c, i):
+            if not live(c):
+                return
+            codes, scales = hs_mx[c]
             bank = psum.tile([P, PACK, P], F32, name="lat_bank", tag="vector_ring")
-            lat_bank[(r, i)] = bank
-            tokens = slice(i * P, (i + 1) * P)
+            lat_bank[(c, i)] = bank
             for t in range(PACK):
-                cols = slice(t * P, (t + 1) * P)
                 nc.tensor.matmul_mx(
                     out=bank[:, t, :],
-                    lhsT=wa_codes[:, cols].bitcast(FP8X4),
-                    lhsT_scale=wa_scales[:, cols],
-                    rhs=codes[:, tokens].bitcast(FP8X4),
-                    rhs_scale=scales[:, tokens],
+                    lhsT=wa_codes[:, columns(t)].bitcast(FP8X4),
+                    lhsT_scale=wa_scales[:, columns(t)],
+                    rhs=codes[:, columns(i)].bitcast(FP8X4),
+                    rhs_scale=scales[:, columns(i)],
                     start=True,
                     stop=True,
                 )
 
-        def latent_out(r, i):
-            if not live(r):
+        def latent_out(c, i):
+            if not live(c):
                 return
             if i == 0:
-                lat_grouped[r] = work.tile(
-                    [P, ROUND, P, PACK], BF16, name="lat_grouped", tag="lat_grouped",
-                    align_bytes=64,
+                lat_grouped[c] = work.tile(
+                    [P, CHUNK * P * PACK], BF16, name="lat_grouped", tag="lat_grouped", align_bytes=64
                 )
             nc.vector.tensor_tensor(
-                out=lat_grouped[r][:, i, :, :],
-                in0=lat_bank[(r, i)][:].rearrange("p t k -> p k t"),
+                out=lat_grouped[c][:].rearrange("p (i k t) -> p i k t", i=CHUNK, t=PACK)[:, i, :, :],
+                in0=lat_bank[(c, i)][:].rearrange("p t k -> p k t"),
                 in1=bias_lat[:].unsqueeze(1).to_broadcast([P, P, PACK]),
                 op=ADD,
             )
 
-        def quantise_latent(r):
-            if not live(r):
+        def quantise_latent(c, halves=(0, 1)):
+            if not live(c):
                 return
-            codes = work.tile([P, ROUND * P], U32, name="lat_codes", tag="lat_codes", align_bytes=64)
-            scales = work.tile(
-                [P, ROUND * P], U8, name="lat_scales", tag="lat_scales", align_bytes=64
-            )
-            nc.vector.quantize_mx(
-                out=codes[:].bitcast(FP8X4),
-                scales=scales[:],
-                in_=lat_grouped[r][:].rearrange("p i k t -> p (i k t)"),
-            )
-            lat_mx[r] = (codes, scales)
+            if halves[0] == 0:
+                codes = work.tile(
+                    [P, CHUNK * P], U32, name="lat_codes", tag="lat_codes", align_bytes=64
+                )
+                scales = work.tile(
+                    [P, CHUNK * P], U8, name="lat_scales", tag="lat_scales", align_bytes=64
+                )
+                lat_mx[c] = (codes, scales)
+            quantise(lat_grouped, lat_mx, c, halves)
 
-        def rope_matmuls(r):
-            if not live(r):
+        def key_matmul(c, half):
+            if not live(c):
                 return
-            codes, scales = hs_mx[r]
-            bank = psum.tile([P, ROUND, ROPE], F32, name="rope_bank", tag="vector_ring")
-            rope_bank[r] = bank
+            codes, scales = hs_mx[c]
+            tokens = columns(half * ROUND, ROUND)
+            bank = psum.tile([P, ROUND * P], F32, name="dim_bank", tag="scalar_ring")
+            nc.tensor.matmul_mx(
+                out=bank[:],
+                lhsT=wa_codes[:, ROPE_COLS].bitcast(FP8X4),
+                lhsT_scale=wa_scales[:, ROPE_COLS],
+                rhs=codes[:, tokens].bitcast(FP8X4),
+                rhs_scale=scales[:, tokens],
+                start=True,
+                stop=True,
+            )
+            key = work.tile([P, ROUND * P], F32, name="key_by_dim", tag="key_by_dim")
+            key_by_dim[(c, half)] = key
+            nc.scalar.activation(out=key[:], in_=bank[:], func=IDENTITY, bias=bias_rope[:])
+
+        def key_transpose(c, half):
+            if not live(c):
+                return
+            if half == 0:
+                key_sin[c] = work.tile([P, CHUNK, ROPE], F32, name="key_sin", tag="key_sin", bufs=1)
+                key_swapped[c] = work.tile([P, CHUNK, ROPE], F32, name="key_swapped", tag="key_swapped", bufs=1)
+            bank = psum.tile([P, ROUND, ROPE], F32, name="key_bank", tag="scalar_ring")
+            key_bank[(c, half)] = bank
             for i in range(ROUND):
-                tokens = slice(i * P, (i + 1) * P)
+                nc.tensor.transpose(bank[:, i, :], key_by_dim[(c, half)][:, columns(i)], ident[:])
+            swapped = key_swapped[c][:, tiles_of(half), :]
+            nc.scalar.mul(swapped[:, :, low], bank[:, :, high], -1.0)
+            nc.scalar.copy(out=swapped[:, :, high], in_=bank[:, :, low])
+
+        def times_cos(c, half):
+            if not live(c):
+                return
+            if half == 0:
+                key_cos[c] = work.tile([P, CHUNK, ROPE], F32, name="key_cos", tag="key_cos")
+            nc.vector.tensor_tensor(
+                out=key_cos[c][:, tiles_of(half), :],
+                in0=key_bank[(c, half)][:],
+                in1=cos_sb[c][:, tiles_of(half), :],
+                op=MUL,
+            )
+
+        def hold_gpsimd(values):
+            nc.vector.memset(values[:, 0, 0:1], 0.0)
+
+        def times_sin(c):
+            if not live(c):
+                return
+            nc.gpsimd.tensor_tensor(out=key_sin[c][:], in0=key_swapped[c][:], in1=sin_sb[c][:], op=MUL)
+            kk_sb[c] = stage.tile([P, HEADS, CHUNK, KK], F32, name="kk_sb", tag="kk_sb")
+
+        def rotated(c, head, tiles=slice(0, CHUNK)):
+            return kk_sb[c][:, head, tiles, ROPE_DIMS]
+
+        def sum_rotation(c, tiles=slice(0, CHUNK)):
+            if not live(c):
+                return
+            nc.gpsimd.tensor_tensor(
+                out=rotated(c, 1, tiles),
+                in0=key_cos[c][:, tiles, :],
+                in1=key_sin[c][:, tiles, :],
+                op=ADD,
+            )
+
+        def copy_rotated(c):
+            if not live(c):
+                return
+            nc.gpsimd.tensor_scalar(
+                out=rotated(c, 0), in0=rotated(c, 1), scalar1=1.0, scalar2=0.0, op0=MUL, op1=ADD
+            )
+
+        def copy_rotated_on_scalar(c, half):
+            here = tiles_of(half)
+            nc.scalar.copy(out=rotated(c, 0, here), in_=rotated(c, 1, here))
+
+        def value_sums(c, pair, copy=nc.scalar.copy):
+            if not live(c):
+                return
+            codes, scales = lat_mx[c]
+            if pair == 0:
+                v_sb[c] = stage.tile([P, HEADS, CHUNK, VDIM], F32, name="v_sb", tag="v_sb")
+            bank = psum.tile([P, 2, HEADS, VDIM], F32, name="v_bank", tag="scalar_ring")
+            for i in range(2):
+                tokens = columns(2 * pair + i)
                 nc.tensor.matmul_mx(
-                    out=bank[:, i, :],
+                    out=bank[:, i, :, :].rearrange("p h d -> p (h d)"),
                     lhsT=codes[:, tokens].bitcast(FP8X4),
                     lhsT_scale=scales[:, tokens],
-                    rhs=wa_codes[:, ROPE_COLS].bitcast(FP8X4),
-                    rhs_scale=wa_scales[:, ROPE_COLS],
+                    rhs=wb_codes[:, V_COLS].bitcast(FP8X4),
+                    rhs_scale=wb_scales[:, V_COLS],
                     start=True,
                     stop=True,
                 )
+            copy(
+                out=v_sb[c][:, :, 2 * pair : 2 * pair + 2, :].rearrange("p h i d -> p i h d"),
+                in_=bank[:],
+            )
 
-        def rope_out(r):
-            if not live(r):
+        def nope_sums(c, half):
+            if not live(c):
                 return
-            c, j = divmod(r * ROUND, CHUNK)
-            if j == 0:
-                rope_key[c] = work.tile([P, CHUNK, ROPE], F32, name="rope_key", tag="rope_key")
-            nc.vector.tensor_tensor(
-                out=rope_key[c][:, j : j + ROUND, :],
-                in0=rope_bank[r][:],
-                in1=bias_rope[:].unsqueeze(1).to_broadcast([P, ROUND, ROPE]),
-                op=ADD,
-            )
-
-        low, high = slice(0, HALF), slice(HALF, ROPE)
-
-        def rotate_products(c):
-            if not 0 <= c < CHUNKS:
-                return
-            key = rope_key[c]
-            key_cos[c] = work.tile([P, CHUNK, ROPE], F32, name="key_cos", tag="key_cos", bufs=1)
-            key_sin[c] = work.tile([P, CHUNK, ROPE], F32, name="key_sin", tag="key_sin", bufs=1)
-            nc.gpsimd.tensor_tensor(out=key_cos[c][:], in0=key[:], in1=cos_sb[c][:], op=MUL)
-            nc.gpsimd.tensor_tensor(
-                out=key_sin[c][:, :, low], in0=key[:, :, high], in1=sin_sb[c][:, :, low], op=MUL
-            )
-            nc.gpsimd.tensor_tensor(
-                out=key_sin[c][:, :, high], in0=key[:, :, low], in1=sin_sb[c][:, :, high], op=MUL
-            )
-
-        def rotate_sum(c):
-            if not 0 <= c < CHUNKS:
-                return
-            kk_sb[c] = stage.tile([P, HEADS, CHUNK, KK], F32, name="kk_sb", tag="kk_sb")
-            nc.vector.tensor_tensor(
-                out=kk_sb[c][:, 1, :, NOPE : NOPE + HALF],
-                in0=key_cos[c][:, :, low],
-                in1=key_sin[c][:, :, low],
-                op=SUB,
-            )
-            nc.vector.tensor_tensor(
-                out=kk_sb[c][:, 1, :, NOPE + HALF :],
-                in0=key_cos[c][:, :, high],
-                in1=key_sin[c][:, :, high],
-                op=ADD,
-            )
-
-        def second_product(r):
-            if not live(r):
-                return
-            codes, scales = lat_mx[r]
-            c, j = divmod(r * ROUND, CHUNK)
-            if j == 0:
-                v_sb[c] = stage.tile([P, HEADS, CHUNK, VDIM], F32, name="v_sb", tag="v_sb")
-            for half in range(ROUND // 2):
-                bank = psum.tile([P, 2, HEADS, VDIM], F32, name="v_bank", tag="scalar_ring")
-                for i in range(2):
-                    tokens = slice((2 * half + i) * P, (2 * half + i + 1) * P)
-                    nc.tensor.matmul_mx(
-                        out=bank[:, i, :, :].rearrange("p h d -> p (h d)"),
-                        lhsT=codes[:, tokens].bitcast(FP8X4),
-                        lhsT_scale=scales[:, tokens],
-                        rhs=wb_codes[:, V_COLS].bitcast(FP8X4),
-                        rhs_scale=wb_scales[:, V_COLS],
-                        start=True,
-                        stop=True,
-                    )
-                first = j + 2 * half
-                nc.scalar.copy(
-                    out=v_sb[c][:, :, first : first + 2, :].rearrange("p h i d -> p i h d"),
-                    in_=bank[:],
-                )
+            codes, scales = lat_mx[c]
             bank = psum.tile([P, ROUND, HEADS, NOPE], F32, name="nope_bank", tag="scalar_ring")
             for i in range(ROUND):
-                tokens = slice(i * P, (i + 1) * P)
+                tokens = columns(half * ROUND + i)
                 nc.tensor.matmul_mx(
                     out=bank[:, i, :, :].rearrange("p h d -> p (h d)"),
                     lhsT=codes[:, tokens].bitcast(FP8X4),
@@ -325,41 +295,210 @@ def tile_gptossmlaattention_pa_t_kernel(
                     start=True,
                     stop=True,
                 )
+            here = tiles_of(half)
             nc.scalar.copy(
-                out=kk_sb[c][:, :, j : j + ROUND, 0:NOPE].rearrange("p h i d -> p i h d"),
-                in_=bank[:],
+                out=kk_sb[c][:, :, here, 0:NOPE].rearrange("p h i d -> p i h d"), in_=bank[:]
             )
-            nc.scalar.copy(
-                out=kk_sb[c][:, 0, j : j + ROUND, NOPE:], in_=kk_sb[c][:, 1, j : j + ROUND, NOPE:]
-            )
-            tiles = slice(r * ROUND, (r + 1) * ROUND)
-            nc.sync.dma_start(out=v_view[:, :, tiles, :], in_=v_sb[c][:, :, j : j + ROUND, :])
-            nc.sync.dma_start(out=kk_view[:, :, tiles, :], in_=kk_sb[c][:, :, j : j + ROUND, :])
 
-        for c in range(-FILL_STEPS, CHUNKS + 1):
-            a, b = 2 * c, 2 * c + 1
-            second_product(a - 2)
-            second_product(b - 2)
-            rotate_products(c)
-            for i in range(ROUND):
-                latent_out(a, i)
-                latent_matmuls(b, i)
-            latent_out(b, 0)
-            rope_matmuls(a + 2)
-            latent_out(b, 1)
-            rope_matmuls(b + 2)
-            latent_out(b, 2)
-            latent_matmuls(a + 2, 0)
-            latent_out(b, 3)
-            latent_matmuls(a + 2, 1)
-            rope_out(a + 2)
-            latent_matmuls(a + 2, 2)
-            rope_out(b + 2)
-            latent_matmuls(a + 2, 3)
-            transpose_hidden(a + 6)
-            transpose_hidden(b + 6)
-            quantise_latent(a)
-            quantise_latent(b)
-            quantise_hidden(a + 4)
-            quantise_hidden(b + 4)
-            rotate_sum(c)
+        def store(view, rows, c, half):
+            if not live(c):
+                return
+            first = c * CHUNK + half * ROUND
+            nc.sync.dma_start(
+                out=view[:, :, first : first + ROUND, :], in_=rows[c][:, :, tiles_of(half), :]
+            )
+
+        def store_round(c, half):
+            store(v_view, v_sb, c, half)
+            store(kk_view, kk_sb, c, half)
+
+        with tc.tile_pool(name="setup", bufs=1) as setup:
+            wa_raw = setup.tile([P, PACK, LATENT + ROPE], BF16, name="wa_raw")
+            nc.sync.dma_start(out=wa_raw[:], in_=Wkva.rearrange("(p j) c -> p j c", j=PACK))
+
+            def load_hidden(r):
+                tiles = slice(r * ROUND, (r + 1) * ROUND)
+                nc.sync.dma_start(out=hs_sb[r][:], in_=hs_view[:, tiles, :])
+
+            wb_raw = setup.tile([P, PACK, HEADS * (NOPE + VDIM)], BF16, name="wb_raw")
+            load_hidden(0)
+            nc.sync.dma_start(out=wb_raw[:], in_=Wkvb.rearrange("(p j) c -> p j c", j=PACK))
+            load_hidden(1)
+            nc.sync.dma_start(
+                out=bias_lat[:], in_=bkva[LAT_COLS].rearrange("(m t) -> m t", t=PACK)
+            )
+            nc.sync.dma_start(out=bias_rope[:], in_=bkva[ROPE_COLS].rearrange("(m t) -> m t", t=1))
+            load_hidden(2)
+            load_hidden(3)
+            for c in range(CHUNKS):
+                tiles = slice(c * CHUNK, (c + 1) * CHUNK)
+                nc.sync.dma_start(out=cos_sb[c][:], in_=cos_view[:, tiles, :])
+                nc.sync.dma_start(out=sin_sb[c][:], in_=sin_view[:, tiles, :])
+                for r in (2 * c + 4, 2 * c + 5):
+                    if r < ROUNDS:
+                        load_hidden(r)
+
+            wa_grp = setup.tile([P, LATENT + ROPE, PACK], BF16, name="wa_grp", align_bytes=64)
+            wb_grp = setup.tile(
+                [P, HEADS * (NOPE + VDIM), PACK], BF16, name="wb_grp", align_bytes=64
+            )
+            for copy, ts in ((nc.vector.tensor_copy, slice(0, 2)), (nc.scalar.copy, slice(2, 4))):
+                copy(
+                    out=wa_grp[:, LAT_COLS, :].rearrange("p (t m) j -> p t m j", t=PACK)[:, ts, :, :],
+                    in_=wa_raw[:, :, LAT_COLS].rearrange("p j (m t) -> p t m j", t=PACK)[:, ts, :, :],
+                )
+            nc.vector.tensor_copy(
+                out=wa_grp[:, ROPE_COLS, :], in_=wa_raw[:, :, ROPE_COLS].rearrange("p j c -> p c j")
+            )
+            for cols in (LAT_COLS, ROPE_COLS):
+                nc.vector.quantize_mx(
+                    out=wa_codes[:, cols].bitcast(FP8X4),
+                    scales=wa_scales[:, cols],
+                    in_=wa_grp[:, cols, :].rearrange("p c j -> p (c j)"),
+                )
+
+            def regroup_wb(cols, source):
+                nc.vector.tensor_copy(
+                    out=wb_grp[:, cols, :].rearrange("p (h c) j -> p h c j", h=HEADS),
+                    in_=wb_raw[:].rearrange("p j (h c) -> p h c j", h=HEADS)[:, :, source, :],
+                )
+
+            def quantise_wb(cols):
+                nc.vector.quantize_mx(
+                    out=wb_codes[:, cols].bitcast(FP8X4),
+                    scales=wb_scales[:, cols],
+                    in_=wb_grp[:, cols, :].rearrange("p c j -> p (c j)"),
+                )
+
+
+            for pair in range(4):
+                transpose_hidden(0, pair)
+            regroup_wb(V_COLS, slice(NOPE, NOPE + VDIM))
+            regroup_wb(NOPE_COLS, slice(0, NOPE))
+            quantise_wb(V_COLS)
+            quantise_wb(NOPE_COLS)
+        stage = ctx.enter_context(tc.tile_pool(name="stage", bufs=3))
+        quantise_hidden(0)
+        for pair in range(4):
+            transpose_hidden(1, pair)
+        latent_matmuls(0, 0)
+        latent_matmuls(0, 1)
+        key_matmul(0, 0)
+        key_matmul(0, 1)
+        latent_matmuls(0, 2)
+        latent_matmuls(0, 3)
+        latent_out(0, 0)
+        latent_out(0, 1)
+        quantise_hidden(1)
+        key_transpose(0, 0)
+        key_transpose(0, 1)
+        times_cos(0, 0)
+        times_cos(0, 1)
+        times_sin(0)
+        sum_rotation(0)
+        latent_matmuls(0, 4)
+        latent_matmuls(0, 5)
+        for pair in range(4):
+            transpose_hidden(2, pair)
+        latent_out(0, 2)
+        key_matmul(1, 0)
+        key_matmul(1, 1)
+        latent_matmuls(0, 6)
+        latent_out(0, 3)
+        latent_matmuls(0, 7)
+        latent_out(0, 4)
+        latent_out(0, 5)
+        key_transpose(1, 0)
+        key_transpose(1, 1)
+        latent_out(0, 6)
+        latent_matmuls(1, 0)
+        latent_out(0, 7)
+        latent_matmuls(1, 1)
+        times_cos(1, 0)
+        times_cos(1, 1)
+        for pair in range(4):
+            transpose_hidden(3, pair)
+        quantise_latent(0)
+        quantise_hidden(2)
+        copy_rotated_on_scalar(0, 0)
+        copy_rotated_on_scalar(0, 1)
+        hold_gpsimd(key_sin[1])
+        times_sin(1)
+        sum_rotation(1)
+        copy_rotated(1)
+
+        for c in range(1, CHUNKS - 1):
+            latent_out(c, 0)
+            latent_matmuls(c, 2)
+            latent_matmuls(c, 3)
+            value_sums(c - 1, 0)
+            key_matmul(c + 1, 0)
+            latent_matmuls(c, 4)
+            latent_out(c, 1)
+            value_sums(c - 1, 1)
+            key_matmul(c + 1, 1)
+            latent_matmuls(c, 5)
+            latent_out(c, 2)
+            nope_sums(c - 1, 0)
+            store_round(c - 1, 0)
+            latent_matmuls(c, 6)
+            latent_out(c, 3)
+            value_sums(c - 1, 2)
+            latent_matmuls(c, 7)
+            latent_out(c, 4)
+            key_transpose(c + 1, 0)
+            key_transpose(c + 1, 1)
+            latent_out(c, 5)
+            value_sums(c - 1, 3)
+            latent_out(c, 6)
+            nope_sums(c - 1, 1)
+            store_round(c - 1, 1)
+            latent_matmuls(c + 1, 0)
+            latent_out(c, 7)
+            latent_matmuls(c + 1, 1)
+            times_cos(c + 1, 0)
+            times_cos(c + 1, 1)
+            for pair in range(CHUNK // 2):
+                transpose_hidden(c + 3, pair)
+            quantise_latent(c)
+            quantise_hidden(c + 2)
+            hold_gpsimd(key_sin[c + 1])
+            times_sin(c + 1)
+            if c + 1 < CHUNKS - 1:
+                sum_rotation(c + 1)
+                copy_rotated(c + 1)
+
+        last = CHUNKS - 1
+        low_tiles, high_tiles = tiles_of(0), tiles_of(1)
+        latent_matmuls(last, 2)
+        latent_matmuls(last, 3)
+        value_sums(last - 1, 0)
+        value_sums(last - 1, 1)
+        nope_sums(last - 1, 0)
+        store_round(last - 1, 0)
+        for i in range(4):
+            latent_out(last, i)
+            latent_matmuls(last, 4 + i)
+        value_sums(last - 1, 2)
+        quantise_latent(last, (0,))
+        hold_gpsimd(rotated(last, 1))
+        sum_rotation(last, low_tiles)
+        sum_rotation(last, high_tiles)
+        value_sums(last - 1, 3)
+        nope_sums(last - 1, 1)
+        store_round(last - 1, 1)
+        for i in range(4, CHUNK):
+            latent_out(last, i)
+        nope_sums(last, 0)
+        copy_rotated_on_scalar(last, 0)
+        store(kk_view, kk_sb, last, 0)
+        value_sums(last, 0)
+        value_sums(last, 1)
+        store(v_view, v_sb, last, 0)
+        copy_rotated_on_scalar(last, 1)
+        quantise_latent(last, (1,))
+        nope_sums(last, 1)
+        store(kk_view, kk_sb, last, 1)
+        value_sums(last, 2, nc.vector.tensor_copy)
+        value_sums(last, 3)
+        store(v_view, v_sb, last, 1)

@@ -8,6 +8,7 @@ BF16 = mybir.dt.bfloat16
 U32 = mybir.dt.uint32
 U8 = mybir.dt.uint8
 FP8X4 = mybir.dt.float8_e4m3fn_x4
+SUB = mybir.AluOpType.subtract
 IDENTITY = mybir.ActivationFunctionType.Identity
 ADD = mybir.AluOpType.add
 MUL = mybir.AluOpType.mult
@@ -72,9 +73,11 @@ def tile_gptossmlaattention_pa_t_kernel(
         lat_bank = {}
         lat_grouped = {}
         lat_mx = {}
+        value_bank = {}
+        dim_bank = {}
         key_by_dim = {}
         key_bank = {}
-        key_swapped = {}
+        key = {}
         key_cos = {}
         key_sin = {}
         kk_sb = {}
@@ -92,7 +95,7 @@ def tile_gptossmlaattention_pa_t_kernel(
         def tiles_of(half):
             return slice(half * ROUND, (half + 1) * ROUND)
 
-        def transpose_hidden(c, pair):
+        def transpose_hidden(c, pair, on_vector=False):
             if not live(c):
                 return
             if pair == 0:
@@ -100,13 +103,16 @@ def tile_gptossmlaattention_pa_t_kernel(
                     [P, CHUNK * P * PACK], BF16, name="hs_grouped", tag="hs_grouped", align_bytes=64
                 )
             words = hs_grouped[c][:].bitcast(F32).rearrange("p (i k u) -> p i k u", i=CHUNK, u=2)
-            bank = psum.tile([P, 2, 2, P], F32, name="hs_bank", tag="scalar_ring")
+            ring, copy = "scalar_ring", nc.scalar.copy
+            if on_vector:
+                ring, copy = "vector_ring", nc.vector.tensor_copy
+            bank = psum.tile([P, 2, 2, P], F32, name="hs_bank", tag=ring)
             for i in range(2):
                 r, j = divmod(c * CHUNK + 2 * pair + i, ROUND)
                 row_words = hs_sb[r][:, j, :].bitcast(F32)
                 for u in range(2):
                     nc.tensor.transpose(bank[:, i, u, :], row_words[:, u : HID // 2 : 2], ident[:])
-            nc.scalar.copy(
+            copy(
                 out=words[:, 2 * pair : 2 * pair + 2, :, :],
                 in_=bank[:].rearrange("p i u k -> p i k u"),
             )
@@ -178,12 +184,13 @@ def tile_gptossmlaattention_pa_t_kernel(
                 lat_mx[c] = (codes, scales)
             quantise(lat_grouped, lat_mx, c, halves)
 
-        def key_matmul(c, half):
+        def key_matmul(c, half, on_vector=False):
             if not live(c):
                 return
             codes, scales = hs_mx[c]
             tokens = columns(half * ROUND, ROUND)
-            bank = psum.tile([P, ROUND * P], F32, name="dim_bank", tag="scalar_ring")
+            bank = psum.tile([P, ROUND * P], F32, name="dim_bank", tag="vector_ring" if on_vector else "scalar_ring")
+            dim_bank[(c, half)] = bank
             nc.tensor.matmul_mx(
                 out=bank[:],
                 lhsT=wa_codes[:, ROPE_COLS].bitcast(FP8X4),
@@ -193,23 +200,29 @@ def tile_gptossmlaattention_pa_t_kernel(
                 start=True,
                 stop=True,
             )
-            key = work.tile([P, ROUND * P], F32, name="key_by_dim", tag="key_by_dim")
-            key_by_dim[(c, half)] = key
-            nc.scalar.activation(out=key[:], in_=bank[:], func=IDENTITY, bias=bias_rope[:])
+            by_dim = work.tile([P, ROUND * P], F32, name="key_by_dim", tag="key_by_dim")
+            key_by_dim[(c, half)] = by_dim
+            if not on_vector:
+                nc.scalar.activation(out=by_dim[:], in_=bank[:], func=IDENTITY, bias=bias_rope[:])
+
+        def key_bias(c, half):
+            if not live(c):
+                return
+            nc.vector.tensor_scalar(
+                out=key_by_dim[(c, half)][:], in0=dim_bank[(c, half)][:], scalar1=bias_rope[:], scalar2=None, op0=ADD
+            )
 
         def key_transpose(c, half):
             if not live(c):
                 return
             if half == 0:
                 key_sin[c] = work.tile([P, CHUNK, ROPE], F32, name="key_sin", tag="key_sin", bufs=1)
-                key_swapped[c] = work.tile([P, CHUNK, ROPE], F32, name="key_swapped", tag="key_swapped", bufs=1)
+                key[c] = work.tile([P, CHUNK, ROPE], F32, name="key", tag="key", bufs=1)
             bank = psum.tile([P, ROUND, ROPE], F32, name="key_bank", tag="scalar_ring")
             key_bank[(c, half)] = bank
             for i in range(ROUND):
                 nc.tensor.transpose(bank[:, i, :], key_by_dim[(c, half)][:, columns(i)], ident[:])
-            swapped = key_swapped[c][:, tiles_of(half), :]
-            nc.scalar.mul(swapped[:, :, low], bank[:, :, high], -1.0)
-            nc.scalar.copy(out=swapped[:, :, high], in_=bank[:, :, low])
+            nc.scalar.copy(out=key[c][:, tiles_of(half), :], in_=bank[:])
 
         def times_cos(c, half):
             if not live(c):
@@ -229,7 +242,13 @@ def tile_gptossmlaattention_pa_t_kernel(
         def times_sin(c):
             if not live(c):
                 return
-            nc.gpsimd.tensor_tensor(out=key_sin[c][:], in0=key_swapped[c][:], in1=sin_sb[c][:], op=MUL)
+            by_half = "p n (h d) -> p n h d"
+            nc.gpsimd.tensor_tensor(
+                out=key_sin[c][:].rearrange(by_half, h=2),
+                in0=key[c][:].rearrange(by_half, h=2)[:, :, ::-1, :],
+                in1=sin_sb[c][:].rearrange(by_half, h=2),
+                op=MUL,
+            )
             kk_sb[c] = stage.tile([P, HEADS, CHUNK, KK], F32, name="kk_sb", tag="kk_sb")
 
         def rotated(c, head, tiles=slice(0, CHUNK)):
@@ -238,31 +257,43 @@ def tile_gptossmlaattention_pa_t_kernel(
         def sum_rotation(c, tiles=slice(0, CHUNK)):
             if not live(c):
                 return
-            nc.gpsimd.tensor_tensor(
-                out=rotated(c, 1, tiles),
-                in0=key_cos[c][:, tiles, :],
-                in1=key_sin[c][:, tiles, :],
-                op=ADD,
-            )
+            for half, op in ((low, SUB), (high, ADD)):
+                nc.gpsimd.tensor_tensor(
+                    out=rotated(c, 1, tiles)[:, :, half],
+                    in0=key_cos[c][:, tiles, half],
+                    in1=key_sin[c][:, tiles, half],
+                    op=op,
+                )
 
-        def copy_rotated(c):
+        def copy_rotated(c, engine_copy, tiles=slice(0, CHUNK)):
+            if not live(c):
+                return
+            engine_copy(out=rotated(c, 0, tiles), in_=rotated(c, 1, tiles))
+
+        def copy_rotated_by_dma(c):
+            if not live(c):
+                return
+            nc.sync.dma_start(out=rotated(c, 0), in_=rotated(c, 1))
+
+        def copy_rotated_on_gpsimd(c, tiles=slice(0, CHUNK)):
             if not live(c):
                 return
             nc.gpsimd.tensor_scalar(
-                out=rotated(c, 0), in0=rotated(c, 1), scalar1=1.0, scalar2=0.0, op0=MUL, op1=ADD
+                out=rotated(c, 0, tiles), in0=rotated(c, 1, tiles), scalar1=1.0, scalar2=0.0, op0=MUL, op1=ADD
             )
 
         def copy_rotated_on_scalar(c, half):
             here = tiles_of(half)
             nc.scalar.copy(out=rotated(c, 0, here), in_=rotated(c, 1, here))
 
-        def value_sums(c, pair, copy=nc.scalar.copy):
+        def value_matmuls(c, pair, ring):
             if not live(c):
                 return
             codes, scales = lat_mx[c]
             if pair == 0:
                 v_sb[c] = stage.tile([P, HEADS, CHUNK, VDIM], F32, name="v_sb", tag="v_sb")
-            bank = psum.tile([P, 2, HEADS, VDIM], F32, name="v_bank", tag="scalar_ring")
+            bank = psum.tile([P, 2, HEADS, VDIM], F32, name="v_bank", tag=ring)
+            value_bank[(c, pair)] = bank
             for i in range(2):
                 tokens = columns(2 * pair + i)
                 nc.tensor.matmul_mx(
@@ -274,10 +305,18 @@ def tile_gptossmlaattention_pa_t_kernel(
                     start=True,
                     stop=True,
                 )
+
+        def value_out(c, pair, copy):
+            if not live(c):
+                return
             copy(
                 out=v_sb[c][:, :, 2 * pair : 2 * pair + 2, :].rearrange("p h i d -> p i h d"),
-                in_=bank[:],
+                in_=value_bank[(c, pair)][:],
             )
+
+        def value_sums(c, pair, copy=nc.scalar.copy):
+            value_matmuls(c, pair, "scalar_ring")
+            value_out(c, pair, copy)
 
         def nope_sums(c, half):
             if not live(c):
@@ -322,8 +361,8 @@ def tile_gptossmlaattention_pa_t_kernel(
 
             wb_raw = setup.tile([P, PACK, HEADS * (NOPE + VDIM)], BF16, name="wb_raw")
             load_hidden(0)
-            nc.sync.dma_start(out=wb_raw[:], in_=Wkvb.rearrange("(p j) c -> p j c", j=PACK))
             load_hidden(1)
+            nc.sync.dma_start(out=wb_raw[:], in_=Wkvb.rearrange("(p j) c -> p j c", j=PACK))
             nc.sync.dma_start(
                 out=bias_lat[:], in_=bkva[LAT_COLS].rearrange("(m t) -> m t", t=PACK)
             )
@@ -371,16 +410,20 @@ def tile_gptossmlaattention_pa_t_kernel(
                 )
 
 
-            for pair in range(4):
-                transpose_hidden(0, pair)
+            transpose_hidden(0, 0)
+            transpose_hidden(0, 1)
+            transpose_hidden(0, 2)
+            transpose_hidden(0, 3)
             regroup_wb(V_COLS, slice(NOPE, NOPE + VDIM))
             regroup_wb(NOPE_COLS, slice(0, NOPE))
             quantise_wb(V_COLS)
             quantise_wb(NOPE_COLS)
         stage = ctx.enter_context(tc.tile_pool(name="stage", bufs=3))
         quantise_hidden(0)
-        for pair in range(4):
-            transpose_hidden(1, pair)
+        transpose_hidden(1, 0)
+        transpose_hidden(1, 1)
+        transpose_hidden(1, 2)
+        transpose_hidden(1, 3)
         latent_matmuls(0, 0)
         latent_matmuls(0, 1)
         key_matmul(0, 0)
@@ -396,10 +439,13 @@ def tile_gptossmlaattention_pa_t_kernel(
         times_cos(0, 1)
         times_sin(0)
         sum_rotation(0)
+        copy_rotated_on_gpsimd(0)
         latent_matmuls(0, 4)
         latent_matmuls(0, 5)
-        for pair in range(4):
-            transpose_hidden(2, pair)
+        transpose_hidden(2, 0)
+        transpose_hidden(2, 1)
+        transpose_hidden(2, 2)
+        transpose_hidden(2, 3)
         latent_out(0, 2)
         key_matmul(1, 0)
         key_matmul(1, 1)
@@ -416,36 +462,37 @@ def tile_gptossmlaattention_pa_t_kernel(
         latent_matmuls(1, 1)
         times_cos(1, 0)
         times_cos(1, 1)
-        for pair in range(4):
-            transpose_hidden(3, pair)
+        transpose_hidden(3, 0)
+        transpose_hidden(3, 1)
+        transpose_hidden(3, 2)
+        transpose_hidden(3, 3)
         quantise_latent(0)
         quantise_hidden(2)
-        copy_rotated_on_scalar(0, 0)
-        copy_rotated_on_scalar(0, 1)
         hold_gpsimd(key_sin[1])
         times_sin(1)
         sum_rotation(1)
-        copy_rotated(1)
 
-        for c in range(1, CHUNKS - 1):
+        for c in range(1, CHUNKS - 2):
             latent_out(c, 0)
             latent_matmuls(c, 2)
             latent_matmuls(c, 3)
             value_sums(c - 1, 0)
             key_matmul(c + 1, 0)
-            latent_matmuls(c, 4)
+            key_matmul(c + 1, 1, True)
             latent_out(c, 1)
             value_sums(c - 1, 1)
-            key_matmul(c + 1, 1)
-            latent_matmuls(c, 5)
+            latent_matmuls(c, 4)
             latent_out(c, 2)
             nope_sums(c - 1, 0)
             store_round(c - 1, 0)
-            latent_matmuls(c, 6)
+            copy_rotated_by_dma(c)
+            latent_matmuls(c, 5)
             latent_out(c, 3)
+            key_bias(c + 1, 1)
             value_sums(c - 1, 2)
-            latent_matmuls(c, 7)
+            latent_matmuls(c, 6)
             latent_out(c, 4)
+            latent_matmuls(c, 7)
             key_transpose(c + 1, 0)
             key_transpose(c + 1, 1)
             latent_out(c, 5)
@@ -458,47 +505,93 @@ def tile_gptossmlaattention_pa_t_kernel(
             latent_matmuls(c + 1, 1)
             times_cos(c + 1, 0)
             times_cos(c + 1, 1)
-            for pair in range(CHUNK // 2):
-                transpose_hidden(c + 3, pair)
+            transpose_hidden(c + 3, 0)
+            transpose_hidden(c + 3, 1)
+            transpose_hidden(c + 3, 2)
+            transpose_hidden(c + 3, 3)
             quantise_latent(c)
             quantise_hidden(c + 2)
             hold_gpsimd(key_sin[c + 1])
             times_sin(c + 1)
-            if c + 1 < CHUNKS - 1:
+            if c + 1 < CHUNKS - 2:
                 sum_rotation(c + 1)
-                copy_rotated(c + 1)
 
-        last = CHUNKS - 1
-        low_tiles, high_tiles = tiles_of(0), tiles_of(1)
-        latent_matmuls(last, 2)
-        latent_matmuls(last, 3)
-        value_sums(last - 1, 0)
-        value_sums(last - 1, 1)
-        nope_sums(last - 1, 0)
-        store_round(last - 1, 0)
-        for i in range(4):
-            latent_out(last, i)
-            latent_matmuls(last, 4 + i)
-        value_sums(last - 1, 2)
-        quantise_latent(last, (0,))
-        hold_gpsimd(rotated(last, 1))
-        sum_rotation(last, low_tiles)
-        sum_rotation(last, high_tiles)
-        value_sums(last - 1, 3)
-        nope_sums(last - 1, 1)
-        store_round(last - 1, 1)
-        for i in range(4, CHUNK):
-            latent_out(last, i)
-        nope_sums(last, 0)
-        copy_rotated_on_scalar(last, 0)
-        store(kk_view, kk_sb, last, 0)
-        value_sums(last, 0)
-        value_sums(last, 1)
-        store(v_view, v_sb, last, 0)
-        copy_rotated_on_scalar(last, 1)
-        quantise_latent(last, (1,))
-        nope_sums(last, 1)
-        store(kk_view, kk_sb, last, 1)
-        value_sums(last, 2, nc.vector.tensor_copy)
-        value_sums(last, 3)
-        store(v_view, v_sb, last, 1)
+        value_sums(5, 0)
+        value_sums(5, 1)
+        latent_out(6, 0)
+        latent_matmuls(6, 2)
+        latent_matmuls(6, 3)
+        nope_sums(5, 0)
+        store_round(5, 0)
+        key_matmul(7, 0)
+        latent_matmuls(6, 4)
+        latent_out(6, 1)
+        value_sums(5, 2)
+        key_matmul(7, 1)
+        latent_matmuls(6, 5)
+        latent_out(6, 2)
+        value_sums(5, 3)
+        latent_matmuls(6, 6)
+        latent_out(6, 3)
+        nope_sums(5, 1)
+        store_round(5, 1)
+        latent_matmuls(6, 7)
+        latent_out(6, 4)
+        quantise_latent(6, (0,))
+        hold_gpsimd(rotated(6, 1))
+        sum_rotation(6)
+        key_transpose(7, 0)
+        key_transpose(7, 1)
+        latent_out(6, 5)
+        value_sums(6, 0)
+        value_sums(6, 1)
+        store(v_view, v_sb, 6, 0)
+        latent_out(6, 6)
+        nope_sums(6, 0)
+        latent_matmuls(7, 0)
+        latent_out(6, 7)
+        latent_matmuls(7, 1)
+        times_cos(7, 0)
+        times_cos(7, 1)
+        copy_rotated_on_scalar(6, 0)
+        store(kk_view, kk_sb, 6, 0)
+        copy_rotated_on_scalar(6, 1)
+        quantise_latent(6, (1,))
+        hold_gpsimd(key_sin[7])
+        times_sin(7)
+        latent_matmuls(7, 2)
+        latent_matmuls(7, 3)
+        value_sums(6, 2)
+        value_sums(6, 3)
+        store(v_view, v_sb, 6, 1)
+        nope_sums(6, 1)
+        store(kk_view, kk_sb, 6, 1)
+        latent_out(7, 0)
+        latent_matmuls(7, 4)
+        latent_out(7, 1)
+        latent_matmuls(7, 5)
+        latent_out(7, 2)
+        latent_matmuls(7, 6)
+        latent_out(7, 3)
+        latent_matmuls(7, 7)
+        latent_out(7, 4)
+        quantise_latent(7, (0,))
+        hold_gpsimd(rotated(7, 1))
+        sum_rotation(7, tiles_of(0))
+        sum_rotation(7, tiles_of(1))
+        latent_out(7, 5)
+        latent_out(7, 6)
+        latent_out(7, 7)
+        value_sums(7, 0)
+        value_sums(7, 1)
+        store(v_view, v_sb, 7, 0)
+        nope_sums(7, 0)
+        copy_rotated_on_scalar(7, 0)
+        store(kk_view, kk_sb, 7, 0)
+        copy_rotated_on_scalar(7, 1)
+        quantise_latent(7, (1,))
+        value_sums(7, 2, nc.vector.tensor_copy)
+        value_sums(7, 3)
+        store(v_view, v_sb, 7, 1)
+        nope_sums(7, 1)
+        store(kk_view, kk_sb, 7, 1)

@@ -55,6 +55,7 @@ def tile_gptossmlaattention_pa_t_kernel(
         cos_sb = [keep.tile([P, CHUNK, ROPE], BF16, name="cos%d" % c) for c in range(CHUNKS)]
         sin_sb = [keep.tile([P, CHUNK, ROPE], BF16, name="sin%d" % c) for c in range(CHUNKS)]
         bias_lat = keep.tile([P, PACK], BF16, name="bias_lat")
+        bias_row = keep.tile([P, ROPE], BF16, name="bias_row")
         bias_rope = keep.tile([P, 1], BF16, name="bias_rope")
         ident = keep.tile([P, P], F32, name="ident")
         wa_codes = keep.tile([P, LATENT + ROPE], U32, name="wa_codes", align_bytes=64)
@@ -215,7 +216,7 @@ def tile_gptossmlaattention_pa_t_kernel(
         def key_transpose(c, half):
             if not live(c):
                 return
-            if half == 0:
+            if c not in key:
                 key_sin[c] = work.tile([P, CHUNK, ROPE], F32, name="key_sin", tag="key_sin", bufs=1)
                 key[c] = work.tile([P, CHUNK, ROPE], F32, name="key", tag="key", bufs=1)
             bank = psum.tile([P, ROUND, ROPE], F32, name="key_bank", tag="scalar_ring")
@@ -227,13 +228,53 @@ def tile_gptossmlaattention_pa_t_kernel(
         def times_cos(c, half):
             if not live(c):
                 return
-            if half == 0:
+            if c not in key_cos:
                 key_cos[c] = work.tile([P, CHUNK, ROPE], F32, name="key_cos", tag="key_cos")
             nc.vector.tensor_tensor(
                 out=key_cos[c][:, tiles_of(half), :],
                 in0=key_bank[(c, half)][:],
                 in1=cos_sb[c][:, tiles_of(half), :],
                 op=MUL,
+            )
+
+        def rope_matmuls(c, half):
+            if not live(c):
+                return
+            codes, scales = hs_mx[c]
+            bank = psum.tile([P, ROUND, ROPE], F32, name="rope_bank", tag="vector_ring")
+            key_bank[(c, half)] = bank
+            for i in range(ROUND):
+                tokens = columns(half * ROUND + i)
+                nc.tensor.matmul_mx(
+                    out=bank[:, i, :],
+                    lhsT=codes[:, tokens].bitcast(FP8X4),
+                    lhsT_scale=scales[:, tokens],
+                    rhs=wa_codes[:, ROPE_COLS].bitcast(FP8X4),
+                    rhs_scale=wa_scales[:, ROPE_COLS],
+                    start=True,
+                    stop=True,
+                )
+
+        def rope_out(c, half):
+            if not live(c):
+                return
+            if c not in key:
+                key_sin[c] = work.tile([P, CHUNK, ROPE], F32, name="key_sin", tag="key_sin", bufs=1)
+                key[c] = work.tile([P, CHUNK, ROPE], F32, name="key", tag="key", bufs=1)
+            nc.vector.tensor_tensor(
+                out=key[c][:, tiles_of(half), :],
+                in0=key_bank[(c, half)][:],
+                in1=bias_row[:].unsqueeze(1).to_broadcast([P, ROUND, ROPE]),
+                op=ADD,
+            )
+
+        def times_cos_on_gpsimd(c, tiles=slice(0, CHUNK)):
+            if not live(c):
+                return
+            if c not in key_cos:
+                key_cos[c] = work.tile([P, CHUNK, ROPE], F32, name="key_cos", tag="key_cos")
+            nc.gpsimd.tensor_tensor(
+                out=key_cos[c][:, tiles, :], in0=key[c][:, tiles, :], in1=cos_sb[c][:, tiles, :], op=MUL
             )
 
         def hold_gpsimd(values):
@@ -254,33 +295,20 @@ def tile_gptossmlaattention_pa_t_kernel(
         def rotated(c, head, tiles=slice(0, CHUNK)):
             return kk_sb[c][:, head, tiles, ROPE_DIMS]
 
-        def sum_rotation(c, tiles=slice(0, CHUNK)):
+        def sum_rotation(c, tiles=slice(0, CHUNK), engine=nc.gpsimd):
             if not live(c):
                 return
-            for half, op in ((low, SUB), (high, ADD)):
-                nc.gpsimd.tensor_tensor(
-                    out=rotated(c, 1, tiles)[:, :, half],
-                    in0=key_cos[c][:, tiles, half],
-                    in1=key_sin[c][:, tiles, half],
-                    op=op,
-                )
-
-        def copy_rotated(c, engine_copy, tiles=slice(0, CHUNK)):
-            if not live(c):
-                return
-            engine_copy(out=rotated(c, 0, tiles), in_=rotated(c, 1, tiles))
-
-        def copy_rotated_by_dma(c):
-            if not live(c):
-                return
-            nc.sync.dma_start(out=rotated(c, 0), in_=rotated(c, 1))
-
-        def copy_rotated_on_gpsimd(c, tiles=slice(0, CHUNK)):
-            if not live(c):
-                return
-            nc.gpsimd.tensor_scalar(
-                out=rotated(c, 0, tiles), in0=rotated(c, 1, tiles), scalar1=1.0, scalar2=0.0, op0=MUL, op1=ADD
+            engine.tensor_tensor(
+                out=rotated(c, 1, tiles),
+                in0=key_cos[c][:, tiles, :],
+                in1=key_sin[c][:, tiles, :],
+                op=ADD,
             )
+
+        def negate_sin(c):
+            if not live(c):
+                return
+            nc.scalar.mul(sin_sb[c][:, :, low], sin_sb[c][:, :, low], -1.0)
 
         def copy_rotated_on_scalar(c, half):
             here = tiles_of(half)
@@ -347,6 +375,22 @@ def tile_gptossmlaattention_pa_t_kernel(
                 out=view[:, :, first : first + ROUND, :], in_=rows[c][:, :, tiles_of(half), :]
             )
 
+        def store_rotated(c):
+            if not live(c):
+                return
+            nc.sync.dma_start(
+                out=kk_view[:, 0, c * CHUNK : (c + 1) * CHUNK, ROPE_DIMS], in_=rotated(c, 1)
+            )
+
+        def store_parts(c, half):
+            if not live(c):
+                return
+            here = tiles_of(half)
+            there = slice(c * CHUNK + half * ROUND, c * CHUNK + (half + 1) * ROUND)
+            store(v_view, v_sb, c, half)
+            nc.sync.dma_start(out=kk_view[:, 1, there, :], in_=kk_sb[c][:, 1, here, :])
+            nc.sync.dma_start(out=kk_view[:, 0, there, 0:NOPE], in_=kk_sb[c][:, 0, here, 0:NOPE])
+
         def store_round(c, half):
             store(v_view, v_sb, c, half)
             store(kk_view, kk_sb, c, half)
@@ -369,6 +413,7 @@ def tile_gptossmlaattention_pa_t_kernel(
             nc.sync.dma_start(out=bias_rope[:], in_=bkva[ROPE_COLS].rearrange("(m t) -> m t", t=1))
             load_hidden(2)
             load_hidden(3)
+            nc.sync.dma_start(out=bias_row[:], in_=bkva[ROPE_COLS].partition_broadcast(P))
             for c in range(CHUNKS):
                 tiles = slice(c * CHUNK, (c + 1) * CHUNK)
                 nc.sync.dma_start(out=cos_sb[c][:], in_=cos_view[:, tiles, :])
@@ -435,11 +480,11 @@ def tile_gptossmlaattention_pa_t_kernel(
         quantise_hidden(1)
         key_transpose(0, 0)
         key_transpose(0, 1)
+        negate_sin(0)
         times_cos(0, 0)
         times_cos(0, 1)
         times_sin(0)
         sum_rotation(0)
-        copy_rotated_on_gpsimd(0)
         latent_matmuls(0, 4)
         latent_matmuls(0, 5)
         transpose_hidden(2, 0)
@@ -456,6 +501,7 @@ def tile_gptossmlaattention_pa_t_kernel(
         latent_out(0, 5)
         key_transpose(1, 0)
         key_transpose(1, 1)
+        negate_sin(1)
         latent_out(0, 6)
         latent_matmuls(1, 0)
         latent_out(0, 7)
@@ -471,39 +517,38 @@ def tile_gptossmlaattention_pa_t_kernel(
         hold_gpsimd(key_sin[1])
         times_sin(1)
         sum_rotation(1)
-
+        store_rotated(0)
         for c in range(1, CHUNKS - 2):
             latent_out(c, 0)
             latent_matmuls(c, 2)
             latent_matmuls(c, 3)
             value_sums(c - 1, 0)
-            key_matmul(c + 1, 0)
-            key_matmul(c + 1, 1, True)
+            key_matmul(c + 1, 1)
+            latent_matmuls(c, 4)
             latent_out(c, 1)
             value_sums(c - 1, 1)
-            latent_matmuls(c, 4)
+            latent_matmuls(c, 5)
             latent_out(c, 2)
             nope_sums(c - 1, 0)
-            store_round(c - 1, 0)
-            copy_rotated_by_dma(c)
-            latent_matmuls(c, 5)
-            latent_out(c, 3)
-            key_bias(c + 1, 1)
-            value_sums(c - 1, 2)
+            negate_sin(c + 1)
+            store_parts(c - 1, 0)
+            store_rotated(c)
             latent_matmuls(c, 6)
-            latent_out(c, 4)
+            latent_out(c, 3)
+            value_sums(c - 1, 2)
             latent_matmuls(c, 7)
-            key_transpose(c + 1, 0)
+            latent_out(c, 4)
             key_transpose(c + 1, 1)
+            rope_matmuls(c + 1, 0)
             latent_out(c, 5)
             value_sums(c - 1, 3)
             latent_out(c, 6)
             nope_sums(c - 1, 1)
-            store_round(c - 1, 1)
+            store_parts(c - 1, 1)
             latent_matmuls(c + 1, 0)
             latent_out(c, 7)
             latent_matmuls(c + 1, 1)
-            times_cos(c + 1, 0)
+            rope_out(c + 1, 0)
             times_cos(c + 1, 1)
             transpose_hidden(c + 3, 0)
             transpose_hidden(c + 3, 1)
@@ -513,16 +558,18 @@ def tile_gptossmlaattention_pa_t_kernel(
             quantise_hidden(c + 2)
             hold_gpsimd(key_sin[c + 1])
             times_sin(c + 1)
+            times_cos_on_gpsimd(c + 1, tiles_of(0))
             if c + 1 < CHUNKS - 2:
                 sum_rotation(c + 1)
 
         value_sums(5, 0)
         value_sums(5, 1)
+        negate_sin(7)
         latent_out(6, 0)
         latent_matmuls(6, 2)
         latent_matmuls(6, 3)
         nope_sums(5, 0)
-        store_round(5, 0)
+        store_parts(5, 0)
         key_matmul(7, 0)
         latent_matmuls(6, 4)
         latent_out(6, 1)
@@ -534,7 +581,7 @@ def tile_gptossmlaattention_pa_t_kernel(
         latent_matmuls(6, 6)
         latent_out(6, 3)
         nope_sums(5, 1)
-        store_round(5, 1)
+        store_parts(5, 1)
         latent_matmuls(6, 7)
         latent_out(6, 4)
         quantise_latent(6, (0,))

from contextlib import ExitStack

import concourse.mybir as mybir
from concourse.masks import make_identity

F32 = mybir.dt.float32
BF16 = mybir.dt.bfloat16
U32 = mybir.dt.uint32
U8 = mybir.dt.uint8
FP8X4 = mybir.dt.float8_e4m3fn_x4
SUB = mybir.AluOpType.subtract
IDENTITY = mybir.ActivationFunctionType.Identity
ADD = mybir.AluOpType.add
MUL = mybir.AluOpType.mult

P = 128
PACK = 4
TOKENS = 8192
HID = 512
LATENT = 512
ROPE = 128
HALF = ROPE // 2
NOPE = 64
VDIM = 128
HEADS = 2
KK = NOPE + ROPE

TILES = TOKENS // P
ROUND = 4
ROUNDS = TILES // ROUND
CHUNK = 2 * ROUND
CHUNKS = TILES // CHUNK
FILL_STEPS = 3

FLOPS = 2 * TOKENS * HID * (LATENT + ROPE) + 2 * TOKENS * LATENT * HEADS * (NOPE + VDIM)


def tile_gptossmlaattention_pa_t_kernel(
    tc, hidden_states, cos, sin, Wkva, bkva, Wkvb, out_0, out_1
):
    nc = tc.nc
    with ExitStack() as ctx:
        keep = ctx.enter_context(tc.tile_pool(name="keep", bufs=1))
        work = ctx.enter_context(tc.tile_pool(name="work", bufs=2))
        psum = ctx.enter_context(tc.psum_pool(name="psum", bufs=4))
        ctx.enter_context(tc.manual_schedule())

        hs_view = hidden_states.flatten_outer_dims().rearrange("(p n) k -> p n k", n=TILES)
        cos_view = cos.flatten_outer_dims().rearrange("(p n) d -> p n d", n=TILES)
        sin_view = sin.flatten_outer_dims().rearrange("(p n) d -> p n d", n=TILES)
        kk_view = out_0.rearrange("b h (p n) d -> p (b h) n d", n=TILES)
        v_view = out_1.rearrange("b h (p n) d -> p (b h) n d", n=TILES)

        hs_sb = [keep.tile([P, ROUND, HID], BF16, name="hs%d" % r) for r in range(ROUNDS)]
        cos_sb = [keep.tile([P, CHUNK, ROPE], BF16, name="cos%d" % c) for c in range(CHUNKS)]
        sin_sb = [keep.tile([P, CHUNK, ROPE], BF16, name="sin%d" % c) for c in range(CHUNKS)]
        bias_lat = keep.tile([P, PACK], BF16, name="bias_lat")
        bias_row = keep.tile([P, ROPE], BF16, name="bias_row")
        bias_rope = keep.tile([P, 1], BF16, name="bias_rope")
        ident = keep.tile([P, P], F32, name="ident")
        wa_codes = keep.tile([P, LATENT + ROPE], U32, name="wa_codes", align_bytes=64)
        wa_scales = keep.tile([P, LATENT + ROPE], U8, name="wa_scales", align_bytes=64)
        wb_codes = keep.tile([P, HEADS * (NOPE + VDIM)], U32, name="wb_codes", align_bytes=64)
        wb_scales = keep.tile([P, HEADS * (NOPE + VDIM)], U8, name="wb_scales", align_bytes=64)
        LAT_COLS = slice(0, LATENT)
        ROPE_COLS = slice(LATENT, LATENT + ROPE)
        V_COLS = slice(0, HEADS * VDIM)
        NOPE_COLS = slice(HEADS * VDIM, HEADS * (VDIM + NOPE))

        make_identity(nc, ident[:])

        hs_grouped = {}
        hs_mx = {}
        lat_bank = {}
        lat_grouped = {}
        lat_mx = {}
        value_bank = {}
        dim_bank = {}
        key_by_dim = {}
        key_bank = {}
        key = {}
        key_cos = {}
        key_sin = {}
        kk_sb = {}
        v_sb = {}

        low, high = slice(0, HALF), slice(HALF, ROPE)
        ROPE_DIMS = slice(NOPE, KK)

        def live(c):
            return 0 <= c < CHUNKS

        def columns(i, count=1):
            return slice(i * P, (i + count) * P)

        def tiles_of(half):
            return slice(half * ROUND, (half + 1) * ROUND)

        def transpose_hidden(c, pair, on_vector=False):
            if not live(c):
                return
            if pair == 0:
                hs_grouped[c] = work.tile(
                    [P, CHUNK * P * PACK], BF16, name="hs_grouped", tag="hs_grouped", align_bytes=64
                )
            words = hs_grouped[c][:].bitcast(F32).rearrange("p (i k u) -> p i k u", i=CHUNK, u=2)
            ring, copy = "scalar_ring", nc.scalar.copy
            if on_vector:
                ring, copy = "vector_ring", nc.vector.tensor_copy
            bank = psum.tile([P, 2, 2, P], F32, name="hs_bank", tag=ring)
            for i in range(2):
                r, j = divmod(c * CHUNK + 2 * pair + i, ROUND)
                row_words = hs_sb[r][:, j, :].bitcast(F32)
                for u in range(2):
                    nc.tensor.transpose(bank[:, i, u, :], row_words[:, u : HID // 2 : 2], ident[:])
            copy(
                out=words[:, 2 * pair : 2 * pair + 2, :, :],
                in_=bank[:].rearrange("p i u k -> p i k u"),
            )

        def quantise(grouped, done, c, halves):
            codes, scales = done[c]
            tokens = slice(halves[0] * ROUND * P, (halves[-1] + 1) * ROUND * P)
            values = slice(tokens.start * PACK, tokens.stop * PACK)
            nc.vector.quantize_mx(
                out=codes[:, tokens].bitcast(FP8X4),
                scales=scales[:, tokens],
                in_=grouped[c][:, values],
            )

        def quantise_hidden(c, halves=(0, 1)):
            if not live(c):
                return
            if halves[0] == 0:
                codes = work.tile(
                    [P, CHUNK * P], U32, name="hs_codes", tag="hs_codes", align_bytes=64
                )
                scales = work.tile(
                    [P, CHUNK * P], U8, name="hs_scales", tag="hs_scales", align_bytes=64
                )
                hs_mx[c] = (codes, scales)
            quantise(hs_grouped, hs_mx, c, halves)

        def latent_matmuls(c, i):
            if not live(c):
                return
            codes, scales = hs_mx[c]
            bank = psum.tile([P, PACK, P], F32, name="lat_bank", tag="vector_ring")
            lat_bank[(c, i)] = bank
            for t in range(PACK):
                nc.tensor.matmul_mx(
                    out=bank[:, t, :],
                    lhsT=wa_codes[:, columns(t)].bitcast(FP8X4),
                    lhsT_scale=wa_scales[:, columns(t)],
                    rhs=codes[:, columns(i)].bitcast(FP8X4),
                    rhs_scale=scales[:, columns(i)],
                    start=True,
                    stop=True,
                )

        def latent_out(c, i):
            if not live(c):
                return
            if i == 0:
                lat_grouped[c] = work.tile(
                    [P, CHUNK * P * PACK], BF16, name="lat_grouped", tag="lat_grouped", align_bytes=64
                )
            nc.vector.tensor_tensor(
                out=lat_grouped[c][:].rearrange("p (i k t) -> p i k t", i=CHUNK, t=PACK)[:, i, :, :],
                in0=lat_bank[(c, i)][:].rearrange("p t k -> p k t"),
                in1=bias_lat[:].unsqueeze(1).to_broadcast([P, P, PACK]),
                op=ADD,
            )

        def quantise_latent(c, halves=(0, 1)):
            if not live(c):
                return
            if halves[0] == 0:
                codes = work.tile(
                    [P, CHUNK * P], U32, name="lat_codes", tag="lat_codes", align_bytes=64
                )
                scales = work.tile(
                    [P, CHUNK * P], U8, name="lat_scales", tag="lat_scales", align_bytes=64
                )
                lat_mx[c] = (codes, scales)
            quantise(lat_grouped, lat_mx, c, halves)

        def key_matmul(c, half, on_vector=False):
            if not live(c):
                return
            codes, scales = hs_mx[c]
            tokens = columns(half * ROUND, ROUND)
            bank = psum.tile([P, ROUND * P], F32, name="dim_bank", tag="vector_ring" if on_vector else "scalar_ring")
            dim_bank[(c, half)] = bank
            nc.tensor.matmul_mx(
                out=bank[:],
                lhsT=wa_codes[:, ROPE_COLS].bitcast(FP8X4),
                lhsT_scale=wa_scales[:, ROPE_COLS],
                rhs=codes[:, tokens].bitcast(FP8X4),
                rhs_scale=scales[:, tokens],
                start=True,
                stop=True,
            )
            by_dim = work.tile([P, ROUND * P], F32, name="key_by_dim", tag="key_by_dim")
            key_by_dim[(c, half)] = by_dim
            if not on_vector:
                nc.scalar.activation(out=by_dim[:], in_=bank[:], func=IDENTITY, bias=bias_rope[:])

        def key_bias(c, half):
            if not live(c):
                return
            nc.vector.tensor_scalar(
                out=key_by_dim[(c, half)][:], in0=dim_bank[(c, half)][:], scalar1=bias_rope[:], scalar2=None, op0=ADD
            )

        def key_transpose(c, half):
            if not live(c):
                return
            if c not in key:
                key_sin[c] = work.tile([P, CHUNK, ROPE], F32, name="key_sin", tag="key_sin", bufs=1)
                key[c] = work.tile([P, CHUNK, ROPE], F32, name="key", tag="key", bufs=1)
            bank = psum.tile([P, ROUND, ROPE], F32, name="key_bank", tag="scalar_ring")
            key_bank[(c, half)] = bank
            for i in range(ROUND):
                nc.tensor.transpose(bank[:, i, :], key_by_dim[(c, half)][:, columns(i)], ident[:])
            nc.scalar.copy(out=key[c][:, tiles_of(half), :], in_=bank[:])

        def times_cos(c, half):
            if not live(c):
                return
            if c not in key_cos:
                key_cos[c] = work.tile([P, CHUNK, ROPE], F32, name="key_cos", tag="key_cos")
            nc.vector.tensor_tensor(
                out=key_cos[c][:, tiles_of(half), :],
                in0=key_bank[(c, half)][:],
                in1=cos_sb[c][:, tiles_of(half), :],
                op=MUL,
            )

        def rope_matmuls(c, half):
            if not live(c):
                return
            codes, scales = hs_mx[c]
            bank = psum.tile([P, ROUND, ROPE], F32, name="rope_bank", tag="vector_ring")
            key_bank[(c, half)] = bank
            for i in range(ROUND):
                tokens = columns(half * ROUND + i)
                nc.tensor.matmul_mx(
                    out=bank[:, i, :],
                    lhsT=codes[:, tokens].bitcast(FP8X4),
                    lhsT_scale=scales[:, tokens],
                    rhs=wa_codes[:, ROPE_COLS].bitcast(FP8X4),
                    rhs_scale=wa_scales[:, ROPE_COLS],
                    start=True,
                    stop=True,
                )

        def rope_out(c, half):
            if not live(c):
                return
            if c not in key:
                key_sin[c] = work.tile([P, CHUNK, ROPE], F32, name="key_sin", tag="key_sin", bufs=1)
                key[c] = work.tile([P, CHUNK, ROPE], F32, name="key", tag="key", bufs=1)
            nc.vector.tensor_tensor(
                out=key[c][:, tiles_of(half), :],
                in0=key_bank[(c, half)][:],
                in1=bias_row[:].unsqueeze(1).to_broadcast([P, ROUND, ROPE]),
                op=ADD,
            )

        def times_cos_on_gpsimd(c, tiles=slice(0, CHUNK)):
            if not live(c):
                return
            if c not in key_cos:
                key_cos[c] = work.tile([P, CHUNK, ROPE], F32, name="key_cos", tag="key_cos")
            nc.gpsimd.tensor_tensor(
                out=key_cos[c][:, tiles, :], in0=key[c][:, tiles, :], in1=cos_sb[c][:, tiles, :], op=MUL
            )

        def hold_gpsimd(values):
            nc.vector.memset(values[:, 0, 0:1], 0.0)

        def times_sin(c):
            if not live(c):
                return
            by_half = "p n (h d) -> p n h d"
            nc.gpsimd.tensor_tensor(
                out=key_sin[c][:].rearrange(by_half, h=2),
                in0=key[c][:].rearrange(by_half, h=2)[:, :, ::-1, :],
                in1=sin_sb[c][:].rearrange(by_half, h=2),
                op=MUL,
            )
            kk_sb[c] = stage.tile([P, HEADS, CHUNK, KK], F32, name="kk_sb", tag="kk_sb")

        def rotated(c, head, tiles=slice(0, CHUNK)):
            return kk_sb[c][:, head, tiles, ROPE_DIMS]

        def sum_rotation(c, tiles=slice(0, CHUNK), engine=nc.gpsimd):
            if not live(c):
                return
            engine.tensor_tensor(
                out=rotated(c, 1, tiles),
                in0=key_cos[c][:, tiles, :],
                in1=key_sin[c][:, tiles, :],
                op=ADD,
            )

        def negate_sin(c):
            if not live(c):
                return
            nc.scalar.mul(sin_sb[c][:, :, low], sin_sb[c][:, :, low], -1.0)

        def copy_rotated_on_scalar(c, half):
            here = tiles_of(half)
            nc.scalar.copy(out=rotated(c, 0, here), in_=rotated(c, 1, here))

        def value_matmuls(c, pair, ring):
            if not live(c):
                return
            codes, scales = lat_mx[c]
            if pair == 0:
                v_sb[c] = stage.tile([P, HEADS, CHUNK, VDIM], F32, name="v_sb", tag="v_sb")
            bank = psum.tile([P, 2, HEADS, VDIM], F32, name="v_bank", tag=ring)
            value_bank[(c, pair)] = bank
            for i in range(2):
                tokens = columns(2 * pair + i)
                nc.tensor.matmul_mx(
                    out=bank[:, i, :, :].rearrange("p h d -> p (h d)"),
                    lhsT=codes[:, tokens].bitcast(FP8X4),
                    lhsT_scale=scales[:, tokens],
                    rhs=wb_codes[:, V_COLS].bitcast(FP8X4),
                    rhs_scale=wb_scales[:, V_COLS],
                    start=True,
                    stop=True,
                )

        def value_out(c, pair, copy):
            if not live(c):
                return
            copy(
                out=v_sb[c][:, :, 2 * pair : 2 * pair + 2, :].rearrange("p h i d -> p i h d"),
                in_=value_bank[(c, pair)][:],
            )

        def value_sums(c, pair, copy=nc.scalar.copy):
            value_matmuls(c, pair, "scalar_ring")
            value_out(c, pair, copy)

        def nope_sums(c, half):
            if not live(c):
                return
            codes, scales = lat_mx[c]
            bank = psum.tile([P, ROUND, HEADS, NOPE], F32, name="nope_bank", tag="scalar_ring")
            for i in range(ROUND):
                tokens = columns(half * ROUND + i)
                nc.tensor.matmul_mx(
                    out=bank[:, i, :, :].rearrange("p h d -> p (h d)"),
                    lhsT=codes[:, tokens].bitcast(FP8X4),
                    lhsT_scale=scales[:, tokens],
                    rhs=wb_codes[:, NOPE_COLS].bitcast(FP8X4),
                    rhs_scale=wb_scales[:, NOPE_COLS],
                    start=True,
                    stop=True,
                )
            here = tiles_of(half)
            nc.scalar.copy(
                out=kk_sb[c][:, :, here, 0:NOPE].rearrange("p h i d -> p i h d"), in_=bank[:]
            )

        def store(view, rows, c, half):
            if not live(c):
                return
            first = c * CHUNK + half * ROUND
            nc.sync.dma_start(
                out=view[:, :, first : first + ROUND, :], in_=rows[c][:, :, tiles_of(half), :]
            )

        def store_rotated(c):
            if not live(c):
                return
            nc.sync.dma_start(
                out=kk_view[:, 0, c * CHUNK : (c + 1) * CHUNK, ROPE_DIMS], in_=rotated(c, 1)
            )

        def store_parts(c, half):
            if not live(c):
                return
            here = tiles_of(half)
            there = slice(c * CHUNK + half * ROUND, c * CHUNK + (half + 1) * ROUND)
            store(v_view, v_sb, c, half)
            nc.sync.dma_start(out=kk_view[:, 1, there, :], in_=kk_sb[c][:, 1, here, :])
            nc.sync.dma_start(out=kk_view[:, 0, there, 0:NOPE], in_=kk_sb[c][:, 0, here, 0:NOPE])

        def store_round(c, half):
            store(v_view, v_sb, c, half)
            store(kk_view, kk_sb, c, half)

        with tc.tile_pool(name="setup", bufs=1) as setup:
            wa_raw = setup.tile([P, PACK, LATENT + ROPE], BF16, name="wa_raw")
            nc.sync.dma_start(out=wa_raw[:], in_=Wkva.rearrange("(p j) c -> p j c", j=PACK))

            def load_hidden(r):
                tiles = slice(r * ROUND, (r + 1) * ROUND)
                nc.sync.dma_start(out=hs_sb[r][:], in_=hs_view[:, tiles, :])

            wb_raw = setup.tile([P, PACK, HEADS * (NOPE + VDIM)], BF16, name="wb_raw")
            load_hidden(0)
            load_hidden(1)
            nc.sync.dma_start(out=wb_raw[:], in_=Wkvb.rearrange("(p j) c -> p j c", j=PACK))
            nc.sync.dma_start(
                out=bias_lat[:], in_=bkva[LAT_COLS].rearrange("(m t) -> m t", t=PACK)
            )
            nc.sync.dma_start(out=bias_rope[:], in_=bkva[ROPE_COLS].rearrange("(m t) -> m t", t=1))
            load_hidden(2)
            load_hidden(3)
            nc.sync.dma_start(out=bias_row[:], in_=bkva[ROPE_COLS].partition_broadcast(P))
            for c in range(CHUNKS):
                tiles = slice(c * CHUNK, (c + 1) * CHUNK)
                nc.sync.dma_start(out=cos_sb[c][:], in_=cos_view[:, tiles, :])
                nc.sync.dma_start(out=sin_sb[c][:], in_=sin_view[:, tiles, :])
                for r in (2 * c + 4, 2 * c + 5):
                    if r < ROUNDS:
                        load_hidden(r)

            wa_grp = setup.tile([P, LATENT + ROPE, PACK], BF16, name="wa_grp", align_bytes=64)
            wb_grp = setup.tile(
                [P, HEADS * (NOPE + VDIM), PACK], BF16, name="wb_grp", align_bytes=64
            )
            for copy, ts in ((nc.vector.tensor_copy, slice(0, 2)), (nc.scalar.copy, slice(2, 4))):
                copy(
                    out=wa_grp[:, LAT_COLS, :].rearrange("p (t m) j -> p t m j", t=PACK)[:, ts, :, :],
                    in_=wa_raw[:, :, LAT_COLS].rearrange("p j (m t) -> p t m j", t=PACK)[:, ts, :, :],
                )
            nc.vector.tensor_copy(
                out=wa_grp[:, ROPE_COLS, :], in_=wa_raw[:, :, ROPE_COLS].rearrange("p j c -> p c j")
            )
            for cols in (LAT_COLS, ROPE_COLS):
                nc.vector.quantize_mx(
                    out=wa_codes[:, cols].bitcast(FP8X4),
                    scales=wa_scales[:, cols],
                    in_=wa_grp[:, cols, :].rearrange("p c j -> p (c j)"),
                )

            def regroup_wb(cols, source):
                nc.vector.tensor_copy(
                    out=wb_grp[:, cols, :].rearrange("p (h c) j -> p h c j", h=HEADS),
                    in_=wb_raw[:].rearrange("p j (h c) -> p h c j", h=HEADS)[:, :, source, :],
                )

            def quantise_wb(cols):
                nc.vector.quantize_mx(
                    out=wb_codes[:, cols].bitcast(FP8X4),
                    scales=wb_scales[:, cols],
                    in_=wb_grp[:, cols, :].rearrange("p c j -> p (c j)"),
                )


            transpose_hidden(0, 0)
            transpose_hidden(0, 1)
            transpose_hidden(0, 2)
            transpose_hidden(0, 3)
            regroup_wb(V_COLS, slice(NOPE, NOPE + VDIM))
            regroup_wb(NOPE_COLS, slice(0, NOPE))
            quantise_wb(V_COLS)
            quantise_wb(NOPE_COLS)
        stage = ctx.enter_context(tc.tile_pool(name="stage", bufs=3))
        quantise_hidden(0)
        transpose_hidden(1, 0)
        transpose_hidden(1, 1)
        transpose_hidden(1, 2)
        transpose_hidden(1, 3)
        latent_matmuls(0, 0)
        latent_matmuls(0, 1)
        key_matmul(0, 0)
        key_matmul(0, 1)
        latent_matmuls(0, 2)
        latent_matmuls(0, 3)
        latent_out(0, 0)
        latent_out(0, 1)
        quantise_hidden(1)
        key_transpose(0, 0)
        key_transpose(0, 1)
        negate_sin(0)
        times_cos(0, 0)
        times_cos(0, 1)
        times_sin(0)
        sum_rotation(0)
        latent_matmuls(0, 4)
        latent_matmuls(0, 5)
        transpose_hidden(2, 0)
        transpose_hidden(2, 1)
        transpose_hidden(2, 2)
        transpose_hidden(2, 3)
        latent_out(0, 2)
        key_matmul(1, 0)
        key_matmul(1, 1)
        latent_matmuls(0, 6)
        latent_out(0, 3)
        latent_matmuls(0, 7)
        latent_out(0, 4)
        latent_out(0, 5)
        key_transpose(1, 0)
        key_transpose(1, 1)
        negate_sin(1)
        latent_out(0, 6)
        latent_matmuls(1, 0)
        latent_out(0, 7)
        latent_matmuls(1, 1)
        times_cos(1, 0)
        times_cos(1, 1)
        transpose_hidden(3, 0)
        transpose_hidden(3, 1)
        transpose_hidden(3, 2)
        transpose_hidden(3, 3)
        quantise_latent(0)
        quantise_hidden(2)
        hold_gpsimd(key_sin[1])
        times_sin(1)
        sum_rotation(1)
        store_rotated(0)
        for c in range(1, CHUNKS - 2):
            latent_out(c, 0)
            latent_matmuls(c, 2)
            latent_matmuls(c, 3)
            value_sums(c - 1, 0)
            key_matmul(c + 1, 1)
            latent_matmuls(c, 4)
            latent_out(c, 1)
            value_sums(c - 1, 1)
            latent_matmuls(c, 5)
            latent_out(c, 2)
            nope_sums(c - 1, 0)
            negate_sin(c + 1)
            store_parts(c - 1, 0)
            store_rotated(c)
            latent_matmuls(c, 6)
            latent_out(c, 3)
            value_sums(c - 1, 2)
            latent_matmuls(c, 7)
            latent_out(c, 4)
            key_transpose(c + 1, 1)
            rope_matmuls(c + 1, 0)
            latent_out(c, 5)
            value_sums(c - 1, 3)
            latent_out(c, 6)
            nope_sums(c - 1, 1)
            store_parts(c - 1, 1)
            latent_matmuls(c + 1, 0)
            latent_out(c, 7)
            latent_matmuls(c + 1, 1)
            rope_out(c + 1, 0)
            times_cos(c + 1, 1)
            transpose_hidden(c + 3, 0)
            transpose_hidden(c + 3, 1)
            transpose_hidden(c + 3, 2)
            transpose_hidden(c + 3, 3)
            quantise_latent(c)
            quantise_hidden(c + 2)
            hold_gpsimd(key_sin[c + 1])
            times_sin(c + 1)
            times_cos_on_gpsimd(c + 1, tiles_of(0))
            if c + 1 < CHUNKS - 2:
                sum_rotation(c + 1)

        value_sums(5, 0)
        value_sums(5, 1)
        negate_sin(7)
        latent_out(6, 0)
        latent_matmuls(6, 2)
        latent_matmuls(6, 3)
        nope_sums(5, 0)
        store_parts(5, 0)
        key_matmul(7, 0)
        latent_matmuls(6, 4)
        latent_out(6, 1)
        value_sums(5, 2)
        key_matmul(7, 1)
        latent_matmuls(6, 5)
        latent_out(6, 2)
        value_sums(5, 3)
        latent_matmuls(6, 6)
        latent_out(6, 3)
        nope_sums(5, 1)
        store_parts(5, 1)
        latent_matmuls(6, 7)
        latent_out(6, 4)
        quantise_latent(6, (0,))
        hold_gpsimd(rotated(6, 1))
        sum_rotation(6)
        key_transpose(7, 0)
        key_transpose(7, 1)
        latent_out(6, 5)
        value_sums(6, 0)
        value_sums(6, 1)
        store(v_view, v_sb, 6, 0)
        latent_out(6, 6)
        nope_sums(6, 0)
        latent_matmuls(7, 0)
        latent_out(6, 7)
        latent_matmuls(7, 1)
        times_cos(7, 0)
        times_cos(7, 1)
        copy_rotated_on_scalar(6, 0)
        store(kk_view, kk_sb, 6, 0)
        copy_rotated_on_scalar(6, 1)
        quantise_latent(6, (1,))
        hold_gpsimd(key_sin[7])
        times_sin(7)
        latent_matmuls(7, 2)
        latent_matmuls(7, 3)
        value_sums(6, 2)
        value_sums(6, 3)
        store(v_view, v_sb, 6, 1)
        nope_sums(6, 1)
        store(kk_view, kk_sb, 6, 1)
        latent_out(7, 0)
        latent_matmuls(7, 4)
        latent_out(7, 1)
        latent_matmuls(7, 5)
        latent_out(7, 2)
        latent_matmuls(7, 6)
        latent_out(7, 3)
        latent_matmuls(7, 7)
        latent_out(7, 4)
        quantise_latent(7, (0,))
        hold_gpsimd(rotated(7, 1))
        sum_rotation(7, tiles_of(0))
        sum_rotation(7, tiles_of(1))
        latent_out(7, 5)
        latent_out(7, 6)
        latent_out(7, 7)
        value_sums(7, 0)
        value_sums(7, 1)
        store(v_view, v_sb, 7, 0)
        nope_sums(7, 0)
        copy_rotated_on_scalar(7, 0)
        store(kk_view, kk_sb, 7, 0)
        copy_rotated_on_scalar(7, 1)
        quantise_latent(7, (1,))
        value_sums(7, 2, nc.vector.tensor_copy)
        value_sums(7, 3)
        store(v_view, v_sb, 7, 1)
        nope_sums(7, 1)
        store(kk_view, kk_sb, 7, 1)
